import numpy as np
import ml_dtypes


def mxq(x, axis, fmt="e4m3"):
    dtype, down = {"e4m3": (ml_dtypes.float8_e4m3fn, 7), "e5m2": (ml_dtypes.float8_e5m2, 14)}[fmt]
    v = np.moveaxis(np.asarray(x, np.float32).astype(ml_dtypes.bfloat16).astype(np.float64), axis, -1)
    blocks = v.reshape(v.shape[:-1] + (-1, 32))
    amax = np.abs(blocks).max(-1, keepdims=True)
    byte = np.maximum(np.where(amax > 0, np.frexp(amax)[1] - 1 + 127, 0) - down, 1)
    scale = np.exp2(byte - 127.0)
    codes = (blocks / scale).astype(np.float32).astype(dtype).astype(np.float64)
    return np.moveaxis((codes * scale).reshape(v.shape), -1, axis)


WIDE = False


def mx_kscale(k):
    if not WIDE:
        return np.ones(k)
    levels = np.array([10, -10, 5, -5, 0])
    a = np.random.permutation(np.resize(levels, k // 512 * 4)).reshape(k // 512, 4)
    idx = np.arange(k)
    return np.exp2(a[idx // 512, idx % 128 // 32])


BF16 = ml_dtypes.bfloat16


def bf(x):
    return np.asarray(x, np.float32).astype(BF16)


def f64(x):
    return np.asarray(x).astype(np.float64)


E2M1 = np.array([0.0, 0.5, 1.0, 1.5, 2.0, 3.0, 4.0, 6.0, -0.0, -0.5, -1.0, -1.5, -2.0, -3.0, -4.0, -6.0])


def pack_weight(w, fmt):
    k, n = w.shape
    w = f64(bf(w)).reshape(k // 32, 32, n)
    amax = np.abs(w).max(1)
    if fmt == "e4m3":
        byte = np.frexp(amax)[1] - 1 + 127 - 7
    else:
        mant, ex = np.frexp(amax / 6.0)
        byte = np.where(mant > 0.5, ex, ex - 1) + 127
    byte = np.clip(np.where(amax > 0, byte, 1), 1, 254)
    scaled = (w * np.exp2(127.0 - byte)[:, None, :]).reshape(k, n).astype(np.float32)
    by_word = np.ascontiguousarray(scaled.reshape(k // 512, 128, 4, n).transpose(0, 1, 3, 2))
    if fmt == "e4m3":
        words = by_word.astype(ml_dtypes.float8_e4m3fn).view(np.uint8)
    else:
        c = by_word.astype(ml_dtypes.float4_e2m1fn).view(np.uint8) & 0xF
        words = c[..., 0::2] | (c[..., 1::2] << 4)
    return np.ascontiguousarray(words), np.ascontiguousarray(byte.astype(np.uint8).reshape(k // 512, 16, n))


def unpack_weight(words, scales, fmt):
    g, p, n, _ = words.shape
    if fmt == "e4m3":
        vals = np.ascontiguousarray(words).view(ml_dtypes.float8_e4m3fn).astype(np.float64)
    else:
        nib = np.empty((g, p, n, 4), np.uint8)
        nib[..., 0::2] = words & 0xF
        nib[..., 1::2] = words >> 4
        vals = E2M1[nib]
    vals = vals * np.repeat(np.exp2(scales.astype(np.float64) - 127.0), 8, axis=1)[..., None]
    return vals.transpose(0, 1, 3, 2).reshape(g * 512, n)

def pack4(w):
    words, scales = pack_weight(w, "e2m1")
    return words.reshape(words.shape[0], 128, -1), scales


def unpack4(words, scales):
    return unpack_weight(words.reshape(words.shape[0], 128, -1, 2), scales, "e2m1")


B, DI, DH = 4096, 1024, 128


def sigmoid(v):
    return 1.0 / (1.0 + np.exp(-v))


def setup_inputs():
    s = mx_kscale(DI)
    n = np.random.standard_normal
    a, c = 0.7 / np.sqrt(DI), 0.7 / np.sqrt(DH)
    keep = np.random.uniform(size=B) < 0.9
    out = {
        "x": bf(n((B, DI)) * s),
        "h_minors": bf(n((B, DH))),
        "c_minors": bf(n((B, DH))),
        "s0": bf(n((B, DH))),
        "s1": bf(n((B, DH))),
        "s2": bf(n((B, DH))),
        "mask": bf(keep * (0.5 + 0.5 * np.random.uniform(size=B))),
    }
    words, scales = pack4((n((7 * DH, DI)) * a / s).T)
    out["weight_ih_words"] = words
    out["weight_ih_scales"] = scales
    out.update({
        "bias_ih": bf(n(7 * DH) * 0.3),
        "weight_hh": bf(n((4 * DH, DH)) * c),
        "bias_hh": bf(n(4 * DH) * 0.3),
        "weight_sh0": bf(n((DH, DH)) * c),
        "bias_sh0": bf(n(DH) * 0.3),
        "weight_sh1": bf(n((DH, DH)) * c),
        "bias_sh1": bf(n(DH) * 0.3),
        "weight_sh2": bf(n((DH, DH)) * c),
        "bias_sh2": bf(n(DH) * 0.3),
    })
    return out


def reference(x, h_minors, c_minors, s0, s1, s2, mask, weight_ih_words, weight_ih_scales, bias_ih, weight_hh, bias_hh,
              weight_sh0, bias_sh0, weight_sh1, bias_sh1, weight_sh2, bias_sh2):
    d = DH
    m = f64(mask)[:, None]

    tmp = (mxq(f64(x), 1, "e4m3") @ unpack4(weight_ih_words, weight_ih_scales)) + f64(bias_ih)
    tmp2 = f64(h_minors) @ f64(weight_hh).T + f64(bias_hh)
    tmp3 = np.concatenate([
        f64(s0) @ f64(weight_sh0).T + f64(bias_sh0),
        f64(s1) @ f64(weight_sh1).T + f64(bias_sh1),
        f64(s2) @ f64(weight_sh2).T + f64(bias_sh2),
    ], axis=1)

    tmp_in, tmp_s = tmp[:, :4 * d], tmp[:, 4 * d:]
    pre = tmp_in + tmp2
    ifo = sigmoid(pre[:, :3 * d])
    c_hat = pre[:, 3 * d:]
    i_g, f_g, o_g = ifo[:, :d], ifo[:, d:2 * d], ifo[:, 2 * d:]

    c_t = (f_g * f64(c_minors) + i_g * np.tanh(c_hat)) * m
    tc = np.tanh(c_t) * m
    h = o_g * tc

    bg = sigmoid(tmp_s + tmp3)
    b0, b1, b2 = bg[:, :d], bg[:, d:2 * d], bg[:, 2 * d:]

    s_0 = (b0 + 1.0 - o_g) * tc
    s_1 = (b1 + 2.0 - o_g - s_0) * 0.5 * tc
    s_2 = (b2 + 3.0 - o_g - (2.0 * s_0 + s_1)) * (1.0 / 3.0) * tc

    return (h, c_t, s_0, s_1, s_2)

@@ -1,0 +1,324 @@
+from contextlib import ExitStack
+
+import concourse.mybir as mybir
+from concourse.masks import make_identity
+
+F32 = mybir.dt.float32
+BF16 = mybir.dt.bfloat16
+I32 = mybir.dt.int32
+U32 = mybir.dt.uint32
+U8 = mybir.dt.uint8
+FP8X4 = mybir.dt.float8_e4m3fn_x4
+FP4X4 = mybir.dt.float4_e2m1fn_x4
+ALU = mybir.AluOpType
+ACT = mybir.ActivationFunctionType
+
+P = 128
+BATCH = 4096
+D_IN = 1024
+D_H = 128
+TILES = BATCH // P
+PAIRS = TILES // 2
+K_PASS = 512
+PASSES = D_IN // K_PASS
+N_CELL = 4 * D_H
+N_SHARE = 3 * D_H
+N_ALL = N_CELL + N_SHARE
+SIDE_CHUNK = 8
+
+FLOPS = 2 * BATCH * (D_IN + D_H) * N_ALL
+
+
+def tile_share_lstm_cell_pa_t_kernel(
+    tc,
+    x,
+    h_minors,
+    c_minors,
+    s0,
+    s1,
+    s2,
+    mask,
+    weight_ih_words,
+    weight_ih_scales,
+    bias_ih,
+    weight_hh,
+    bias_hh,
+    weight_sh0,
+    bias_sh0,
+    weight_sh1,
+    bias_sh1,
+    weight_sh2,
+    bias_sh2,
+    out_0,
+    out_1,
+    out_2,
+    out_3,
+    out_4,
+):
+    nc = tc.nc
+    x_rows = x.rearrange("(p j) k -> p j k", j=TILES)
+    side_rows = [a.rearrange("(p j) d -> p j d", j=TILES) for a in (h_minors, s0, s1, s2, c_minors)]
+    out_rows = [a.rearrange("(p j) d -> p j d", j=TILES) for a in (out_0, out_1, out_2, out_3, out_4)]
+
+    with ExitStack() as ctx:
+        keep = ctx.enter_context(tc.tile_pool(name="keep", bufs=1))
+
+        w_words = keep.tile([P, PASSES, 2 * N_ALL], U8, align_bytes=64)
+        nc.sync.dma_start(
+            out=w_words[:].bitcast(I32),
+            in_=weight_ih_words.rearrange("g p b -> p g b").bitcast(I32),
+        )
+        w_scales = keep.tile([P, PASSES, N_ALL], U8, align_bytes=64)
+        nc.vector.memset(w_scales[:].bitcast(I32), 0)
+        for quadrant in range(4):
+            nc.sync.dma_start(
+                out=w_scales[32 * quadrant : 32 * quadrant + 4, :, :].bitcast(I32),
+                in_=weight_ih_scales[:, 4 * quadrant : 4 * quadrant + 4, :]
+                .rearrange("g r n -> r g n")
+                .bitcast(I32),
+            )
+
+        w_small_rows = keep.tile([P, 7, D_H], BF16)
+        nc.sync.dma_start(out=w_small_rows[:, 0:4, :], in_=weight_hh.rearrange("(b c) k -> c b k", c=P))
+        for b, w_sh in enumerate((weight_sh0, weight_sh1, weight_sh2)):
+            nc.sync.dma_start(out=w_small_rows[:, 4 + b, :], in_=w_sh)
+
+        bias_rows = keep.tile([P, N_ALL], BF16)
+        nc.vector.memset(bias_rows[:], 0.0)
+        nc.sync.dma_start(out=bias_rows[0:1, :], in_=bias_ih.unsqueeze(0))
+        nc.sync.dma_start(out=bias_rows[1:2, 0:N_CELL], in_=bias_hh.unsqueeze(0))
+        for b, b_sh in enumerate((bias_sh0, bias_sh1, bias_sh2)):
+            nc.sync.dma_start(
+                out=bias_rows[1:2, N_CELL + D_H * b : N_CELL + D_H * (b + 1)], in_=b_sh.unsqueeze(0)
+            )
+
+        mask_bf = keep.tile([P, TILES], BF16)
+        nc.sync.dma_start(out=mask_bf[:], in_=mask.rearrange("(p j) -> p j", j=TILES))
+        mask_f32 = keep.tile([P, TILES], F32)
+        nc.vector.tensor_copy(out=mask_f32[:], in_=mask_bf[:])
+
+        ident_bf = keep.tile([P, P], BF16)
+        make_identity(nc, ident_bf[:])
+        ident_f32 = keep.tile([P, P], F32)
+        make_identity(nc, ident_f32[:])
+        ones = keep.tile([P, P], BF16)
+        nc.vector.memset(ones[:], 1.0)
+
+        w_small = keep.tile([P, N_ALL], BF16)
+        bias_all = keep.tile([P, N_ALL], F32)
+        with tc.psum_pool(name="setup_psum", bufs=1) as setup_psum:
+            w_small_ps = setup_psum.tile([P, 7, D_H], BF16)
+            for b in range(7):
+                nc.tensor.transpose(w_small_ps[:, b, :], w_small_rows[:, b, :], ident_bf[:])
+            nc.scalar.copy(out=w_small[:], in_=w_small_ps[:].rearrange("k b c -> k (b c)"))
+            bias_cell_ps = setup_psum.tile([P, N_CELL], F32)
+            nc.tensor.matmul(bias_cell_ps[:], lhsT=ones[:], rhs=bias_rows[:, 0:N_CELL], start=True, stop=True)
+            nc.vector.tensor_copy(out=bias_all[:, 0:N_CELL], in_=bias_cell_ps[:])
+            bias_share_ps = setup_psum.tile([P, N_SHARE], F32)
+            nc.tensor.matmul(bias_share_ps[:], lhsT=ones[:], rhs=bias_rows[:, N_CELL:N_ALL], start=True, stop=True)
+            nc.vector.tensor_copy(out=bias_all[:, N_CELL:N_ALL], in_=bias_share_ps[:])
+
+        side = [keep.tile([P, TILES, D_H], BF16, name="side%d" % w) for w in range(5)]
+
+        x_pool = ctx.enter_context(tc.tile_pool(name="x_pool", bufs=4))
+        stage = ctx.enter_context(tc.tile_pool(name="stage", bufs=4))
+        work = ctx.enter_context(tc.tile_pool(name="work", bufs=3))
+        pre_pool = ctx.enter_context(tc.tile_pool(name="pre_pool", bufs=2))
+        late = ctx.enter_context(tc.tile_pool(name="late", bufs=4))
+        psum1 = ctx.enter_context(tc.psum_pool(name="psum1", bufs=1))
+        psum2 = ctx.enter_context(tc.psum_pool(name="psum2", bufs=2))
+
+        x_of = {}
+        hst_of = {}
+        grouped_of = {}
+        codes_of = {}
+        scales_of = {}
+        lin_of = {}
+        pre_of = {}
+        gates_of = {}
+        diff_of = {}
+        tc_of = {}
+
+        def load(k):
+            if (2 * k) % SIDE_CHUNK == 0:
+                rows = slice(2 * k, 2 * k + SIDE_CHUNK)
+                for w in range(5):
+                    nc.sync.dma_start(out=side[w][:, rows, :], in_=side_rows[w][:, rows, :])
+            x_sb = x_pool.tile([P, 2, D_IN], BF16)
+            nc.sync.dma_start(out=x_sb[:], in_=x_rows[:, 2 * k : 2 * k + 2, :])
+            x_of[k] = x_sb
+
+        def front(k):
+            hst_ps = psum1.tile([P, 2, 4, P], BF16)
+            for jj in range(2):
+                for w in range(4):
+                    nc.tensor.transpose(hst_ps[:, jj, w, :], side[w][:, 2 * k + jj, :], ident_bf[:])
+            hst = stage.tile([P, 2, 4, P], BF16)
+            nc.scalar.copy(out=hst[:], in_=hst_ps[:])
+            hst_of[k] = hst
+            grouped = stage.tile([P, 2, PASSES, P, 4], BF16, align_bytes=64)
+            for jj in range(2):
+                x_words = x_of[k][:, jj, :].bitcast(F32)
+                xt_ps = psum2.tile([P, PASSES, 2, P], F32)
+                for g in range(PASSES):
+                    for u in range(2):
+                        nc.tensor.transpose(
+                            xt_ps[:, g, u, :], x_words[:, 256 * g + u : 256 * (g + 1) : 2], ident_f32[:]
+                        )
+                nc.scalar.copy(
+                    out=grouped[:, jj].bitcast(F32), in_=xt_ps[:].rearrange("p g u r -> p g r u")
+                )
+            grouped_of[k] = grouped
+
+        def new_codes(k):
+            codes = work.tile([P, 2, PASSES, P], U32, align_bytes=64)
+            scales = work.tile([P, 2, PASSES, P], U8, align_bytes=64)
+            codes_of[k] = codes
+            scales_of[k] = scales
+
+        def quantise(k, jj):
+            nc.vector.quantize_mx(
+                out=codes_of[k][:, jj].rearrange("p g r -> p (g r)").bitcast(FP8X4),
+                scales=scales_of[k][:, jj].rearrange("p g r -> p (g r)"),
+                in_=grouped_of[k][:, jj].rearrange("p g r t -> p (g r t)"),
+            )
+
+        def small_products(k, jj):
+            if jj == 0:
+                lin = work.tile([P, 2, N_ALL], F32)
+                lin_of[k] = lin
+            lin = lin_of[k]
+            hst = hst_of[k]
+            cell_ps = psum1.tile([P, N_CELL], F32)
+            nc.tensor.matmul(cell_ps[:], lhsT=hst[:, jj, 0, :], rhs=w_small[:, 0:N_CELL], start=True, stop=True)
+            share_ps = psum1.tile([P, N_SHARE], F32)
+            for b in range(3):
+                cols = slice(D_H * b, D_H * (b + 1))
+                nc.tensor.matmul(
+                    share_ps[:, cols],
+                    lhsT=hst[:, jj, 1 + b, :],
+                    rhs=w_small[:, N_CELL + D_H * b : N_CELL + D_H * (b + 1)],
+                    start=True,
+                    stop=True,
+                )
+            nc.vector.tensor_tensor(out=lin[:, jj, 0:N_CELL], in0=cell_ps[:], in1=bias_all[:, 0:N_CELL], op=ALU.add)
+            nc.vector.tensor_tensor(
+                out=lin[:, jj, N_CELL:N_ALL], in0=share_ps[:], in1=bias_all[:, N_CELL:N_ALL], op=ALU.add
+            )
+
+        def mx_group(acc, k, jj, first, width):
+            for g in range(PASSES):
+                nc.tensor.matmul_mx(
+                    out=acc,
+                    lhsT=codes_of[k][:, jj, g, :].bitcast(FP8X4),
+                    lhsT_scale=scales_of[k][:, jj, g, :],
+                    rhs=w_words[:, g, 2 * first : 2 * (first + width)].bitcast(FP4X4),
+                    rhs_scale=w_scales[:, g, first : first + width],
+                    start=(g == 0),
+                    stop=(g == PASSES - 1),
+                )
+
+        def big_product(k, jj):
+            if jj == 0:
+                pre = pre_pool.tile([P, 2, N_ALL], F32)
+                gates = late.tile([P, 2, N_ALL], F32)
+                pre_of[k] = pre
+                gates_of[k] = gates
+            pre = pre_of[k]
+            gates = gates_of[k]
+            lin = lin_of[k]
+            mx_cell_ps = psum2.tile([P, N_CELL], F32)
+            mx_group(mx_cell_ps[:], k, jj, 0, N_CELL)
+            mx_share_ps = psum1.tile([P, N_SHARE], F32)
+            for b in range(3):
+                mx_group(mx_share_ps[:, D_H * b : D_H * (b + 1)], k, jj, N_CELL + D_H * b, D_H)
+            nc.vector.tensor_tensor(out=pre[:, jj, 0:N_CELL], in0=mx_cell_ps[:], in1=lin[:, jj, 0:N_CELL], op=ALU.add)
+            nc.vector.tensor_tensor(
+                out=pre[:, jj, N_CELL:N_ALL], in0=mx_share_ps[:], in1=lin[:, jj, N_CELL:N_ALL], op=ALU.add
+            )
+            nc.scalar.activation(out=gates[:, jj, 0 : 3 * D_H], in_=pre[:, jj, 0 : 3 * D_H], func=ACT.Sigmoid)
+            nc.scalar.activation(out=gates[:, jj, 3 * D_H : N_CELL], in_=pre[:, jj, 3 * D_H : N_CELL], func=ACT.Tanh)
+            nc.scalar.activation(out=gates[:, jj, N_CELL:N_ALL], in_=pre[:, jj, N_CELL:N_ALL], func=ACT.Sigmoid)
+
+        def cell(k):
+            gates = gates_of[k]
+            gate = [gates[:, :, D_H * b : D_H * (b + 1)] for b in range(7)]
+            in_part = work.tile([P, 2, D_H], F32)
+            nc.gpsimd.tensor_tensor(out=in_part[:], in0=gate[0], in1=gate[3], op=ALU.mult)
+            keep_part = work.tile([P, 2, D_H], F32)
+            nc.gpsimd.tensor_tensor(out=keep_part[:], in0=gate[1], in1=side[4][:, 2 * k : 2 * k + 2, :], op=ALU.mult)
+            c_raw = work.tile([P, 2, D_H], F32)
+            nc.gpsimd.tensor_tensor(out=c_raw[:], in0=in_part[:], in1=keep_part[:], op=ALU.add)
+            diff = late.tile([P, 3, 2, D_H], F32)
+            for b in range(3):
+                nc.gpsimd.tensor_tensor(out=diff[:, b], in0=gate[4 + b], in1=gate[2], op=ALU.subtract)
+            diff_of[k] = diff
+            c_t = late.tile([P, 2, D_H], F32)
+            tanh_c = work.tile([P, 2, D_H], F32)
+            tc_m = late.tile([P, 2, D_H], F32)
+            for jj in range(2):
+                m = mask_f32[:, 2 * k + jj : 2 * k + jj + 1]
+                nc.scalar.activation(out=tanh_c[:, jj, :], in_=c_raw[:, jj, :], func=ACT.Tanh, scale=m)
+                nc.scalar.activation(out=c_t[:, jj, :], in_=c_raw[:, jj, :], func=ACT.Copy, scale=m)
+                nc.scalar.activation(out=tc_m[:, jj, :], in_=tanh_c[:, jj, :], func=ACT.Copy, scale=m)
+            nc.sync.dma_start(out=out_rows[1][:, 2 * k : 2 * k + 2, :], in_=c_t[:])
+            tc_of[k] = tc_m
+
+        def tail(k, next_k):
+            o_gate = gates_of[k][:, :, 2 * D_H : 3 * D_H]
+            diff = diff_of[k]
+            tc_m = tc_of[k]
+            rows = slice(2 * k, 2 * k + 2)
+            s_0 = late.tile([P, 2, D_H], F32)
+            nc.vector.scalar_tensor_tensor(out=s_0[:], in0=diff[:, 0], scalar=1.0, in1=tc_m[:], op0=ALU.add, op1=ALU.mult)
+            h_t = late.tile([P, 2, D_H], F32)
+            nc.vector.tensor_tensor(out=h_t[:], in0=o_gate, in1=tc_m[:], op=ALU.mult)
+            rest_1 = work.tile([P, 2, D_H], F32)
+            nc.vector.scalar_tensor_tensor(out=rest_1[:], in0=diff[:, 1], scalar=2.0, in1=s_0[:], op0=ALU.add, op1=ALU.subtract)
+            rest_2 = work.tile([P, 2, D_H], F32)
+            nc.vector.scalar_tensor_tensor(out=rest_2[:], in0=s_0[:], scalar=-2.0, in1=diff[:, 2], op0=ALU.mult, op1=ALU.add)
+            s_1 = late.tile([P, 2, D_H], F32)
+            nc.vector.scalar_tensor_tensor(out=s_1[:], in0=rest_1[:], scalar=0.5, in1=tc_m[:], op0=ALU.mult, op1=ALU.mult)
+            if next_k < PAIRS:
+                quantise(next_k, 0)
+            rest_3 = work.tile([P, 2, D_H], F32)
+            nc.vector.scalar_tensor_tensor(out=rest_3[:], in0=rest_2[:], scalar=3.0, in1=s_1[:], op0=ALU.add, op1=ALU.subtract)
+            if next_k < PAIRS:
+                quantise(next_k, 1)
+            s_2 = late.tile([P, 2, D_H], F32)
+            nc.vector.scalar_tensor_tensor(out=s_2[:], in0=rest_3[:], scalar=1.0 / 3.0, in1=tc_m[:], op0=ALU.mult, op1=ALU.mult)
+            nc.sync.dma_start(out=out_rows[0][:, rows, :], in_=h_t[:])
+            nc.sync.dma_start(out=out_rows[2][:, rows, :], in_=s_0[:])
+            nc.sync.dma_start(out=out_rows[3][:, rows, :], in_=s_1[:])
+            nc.sync.dma_start(out=out_rows[4][:, rows, :], in_=s_2[:])
+
+        ctx.enter_context(tc.manual_schedule())
+        for k in range(4):
+            load(k)
+        for k in range(3):
+            front(k)
+        for k in range(2):
+            new_codes(k)
+            quantise(k, 0)
+            quantise(k, 1)
+        small_products(0, 0)
+        small_products(0, 1)
+        for n in range(PAIRS + 2):
+            if n + 4 < PAIRS:
+                load(n + 4)
+            for jj in range(2):
+                if n + 1 < PAIRS:
+                    small_products(n + 1, jj)
+                if n < PAIRS:
+                    big_product(n, jj)
+            if n + 3 < PAIRS:
+                front(n + 3)
+            if n + 2 < PAIRS:
+                new_codes(n + 2)
+            if 1 <= n <= PAIRS:
+                cell(n - 1)
+            if n >= 2:
+                tail(n - 2, n + 2)
+            elif n + 2 < PAIRS:
+                quantise(n + 2, 0)
+                quantise(n + 2, 1)

@@ -105,7 +105,7 @@ def tile_share_lstm_cell_pa_t_kernel(
         nc.vector.memset(ones[:], 1.0)
 
         w_small = keep.tile([P, N_ALL], BF16)
-        bias_all = keep.tile([P, N_ALL], F32)
+        bias_cell = keep.tile([P, N_CELL], F32)
         with tc.psum_pool(name="setup_psum", bufs=1) as setup_psum:
             w_small_ps = setup_psum.tile([P, 7, D_H], BF16)
             for b in range(7):
@@ -113,10 +113,7 @@ def tile_share_lstm_cell_pa_t_kernel(
             nc.scalar.copy(out=w_small[:], in_=w_small_ps[:].rearrange("k b c -> k (b c)"))
             bias_cell_ps = setup_psum.tile([P, N_CELL], F32)
             nc.tensor.matmul(bias_cell_ps[:], lhsT=ones[:], rhs=bias_rows[:, 0:N_CELL], start=True, stop=True)
-            nc.vector.tensor_copy(out=bias_all[:, 0:N_CELL], in_=bias_cell_ps[:])
-            bias_share_ps = setup_psum.tile([P, N_SHARE], F32)
-            nc.tensor.matmul(bias_share_ps[:], lhsT=ones[:], rhs=bias_rows[:, N_CELL:N_ALL], start=True, stop=True)
-            nc.vector.tensor_copy(out=bias_all[:, N_CELL:N_ALL], in_=bias_share_ps[:])
+            nc.vector.tensor_copy(out=bias_cell[:], in_=bias_cell_ps[:])
 
         side = [keep.tile([P, TILES, D_H], BF16, name="side%d" % w) for w in range(5)]
 
@@ -193,18 +190,12 @@ def tile_share_lstm_cell_pa_t_kernel(
             nc.tensor.matmul(cell_ps[:], lhsT=hst[:, jj, 0, :], rhs=w_small[:, 0:N_CELL], start=True, stop=True)
             share_ps = psum1.tile([P, N_SHARE], F32)
             for b in range(3):
-                cols = slice(D_H * b, D_H * (b + 1))
-                nc.tensor.matmul(
-                    share_ps[:, cols],
-                    lhsT=hst[:, jj, 1 + b, :],
-                    rhs=w_small[:, N_CELL + D_H * b : N_CELL + D_H * (b + 1)],
-                    start=True,
-                    stop=True,
-                )
-            nc.vector.tensor_tensor(out=lin[:, jj, 0:N_CELL], in0=cell_ps[:], in1=bias_all[:, 0:N_CELL], op=ALU.add)
-            nc.vector.tensor_tensor(
-                out=lin[:, jj, N_CELL:N_ALL], in0=share_ps[:], in1=bias_all[:, N_CELL:N_ALL], op=ALU.add
-            )
+                cols = slice(N_CELL + D_H * b, N_CELL + D_H * (b + 1))
+                acc = share_ps[:, D_H * b : D_H * (b + 1)]
+                nc.tensor.matmul(acc, lhsT=ones[:], rhs=bias_rows[:, cols], start=True, stop=False)
+                nc.tensor.matmul(acc, lhsT=hst[:, jj, 1 + b, :], rhs=w_small[:, cols], start=False, stop=True)
+            nc.vector.tensor_tensor(out=lin[:, jj, 0:N_CELL], in0=cell_ps[:], in1=bias_cell[:], op=ALU.add)
+            nc.scalar.copy(out=lin[:, jj, N_CELL:N_ALL], in_=share_ps[:])
 
         def mx_group(acc, k, jj, first, width):
             for g in range(PASSES):

@@ -24,7 +24,7 @@ PASSES = D_IN // K_PASS
 N_CELL = 4 * D_H
 N_SHARE = 3 * D_H
 N_ALL = N_CELL + N_SHARE
-SIDE_CHUNK = 8
+SIDE_CHUNK = 4
 
 FLOPS = 2 * BATCH * (D_IN + D_H) * N_ALL
 
@@ -61,7 +61,44 @@ def tile_share_lstm_cell_pa_t_kernel(
     out_rows = [a.rearrange("(p j) d -> p j d", j=TILES) for a in (out_0, out_1, out_2, out_3, out_4)]
 
     with ExitStack() as ctx:
+        ctx.enter_context(tc.manual_schedule())
         keep = ctx.enter_context(tc.tile_pool(name="keep", bufs=1))
+        x_pool = ctx.enter_context(tc.tile_pool(name="x_pool", bufs=4))
+        stage = ctx.enter_context(tc.tile_pool(name="stage", bufs=4))
+        work = ctx.enter_context(tc.tile_pool(name="work", bufs=3))
+        pre_pool = ctx.enter_context(tc.tile_pool(name="pre_pool", bufs=2))
+        mx_banks = ctx.enter_context(tc.psum_pool(name="mx_banks", bufs=4))
+        plain_banks = ctx.enter_context(tc.psum_pool(name="plain_banks", bufs=4))
+
+        side = [keep.tile([P, TILES, D_H], BF16, name="side%d" % w) for w in range(5)]
+
+        x_of = {}
+        hst_of = {}
+        grouped_of = {}
+        codes_of = {}
+        scales_of = {}
+        lin_of = {}
+        cell_ps_of = {}
+        mx_ps_of = {}
+        gates_of = {}
+        diff_of = {}
+        tc_of = {}
+
+        def load(k):
+            x_sb = x_pool.tile([P, 2, D_IN], BF16)
+            nc.sync.dma_start(out=x_sb[:], in_=x_rows[:, 2 * k : 2 * k + 2, :])
+            x_of[k] = x_sb
+            if (2 * k) % SIDE_CHUNK == 0:
+                rows = slice(2 * k, 2 * k + SIDE_CHUNK)
+                for w in range(5):
+                    nc.sync.dma_start(out=side[w][:, rows, :], in_=side_rows[w][:, rows, :])
+
+        w_small_rows = keep.tile([P, 7, D_H], BF16)
+        nc.scalar.dma_start(out=w_small_rows[:, 0:4, :], in_=weight_hh.rearrange("(b c) k -> c b k", c=P))
+        for b, w_sh in enumerate((weight_sh0, weight_sh1, weight_sh2)):
+            nc.scalar.dma_start(out=w_small_rows[:, 4 + b, :], in_=w_sh)
+
+        load(0)
 
         w_words = keep.tile([P, PASSES, 2 * N_ALL], U8, align_bytes=64)
         nc.sync.dma_start(
@@ -78,75 +115,42 @@ def tile_share_lstm_cell_pa_t_kernel(
                 .bitcast(I32),
             )
 
-        w_small_rows = keep.tile([P, 7, D_H], BF16)
-        nc.sync.dma_start(out=w_small_rows[:, 0:4, :], in_=weight_hh.rearrange("(b c) k -> c b k", c=P))
-        for b, w_sh in enumerate((weight_sh0, weight_sh1, weight_sh2)):
-            nc.sync.dma_start(out=w_small_rows[:, 4 + b, :], in_=w_sh)
-
         bias_rows = keep.tile([P, N_ALL], BF16)
         nc.vector.memset(bias_rows[:], 0.0)
-        nc.sync.dma_start(out=bias_rows[0:1, :], in_=bias_ih.unsqueeze(0))
-        nc.sync.dma_start(out=bias_rows[1:2, 0:N_CELL], in_=bias_hh.unsqueeze(0))
+        nc.scalar.dma_start(out=bias_rows[0:1, :], in_=bias_ih.unsqueeze(0))
+        nc.scalar.dma_start(out=bias_rows[1:2, 0:N_CELL], in_=bias_hh.unsqueeze(0))
         for b, b_sh in enumerate((bias_sh0, bias_sh1, bias_sh2)):
-            nc.sync.dma_start(
+            nc.scalar.dma_start(
                 out=bias_rows[1:2, N_CELL + D_H * b : N_CELL + D_H * (b + 1)], in_=b_sh.unsqueeze(0)
             )
-
-        mask_bf = keep.tile([P, TILES], BF16)
-        nc.sync.dma_start(out=mask_bf[:], in_=mask.rearrange("(p j) -> p j", j=TILES))
-        mask_f32 = keep.tile([P, TILES], F32)
-        nc.vector.tensor_copy(out=mask_f32[:], in_=mask_bf[:])
-
-        ident_bf = keep.tile([P, P], BF16)
-        make_identity(nc, ident_bf[:])
-        ident_f32 = keep.tile([P, P], F32)
-        make_identity(nc, ident_f32[:])
         ones = keep.tile([P, P], BF16)
         nc.vector.memset(ones[:], 1.0)
 
+        ident_f32 = keep.tile([P, P], F32)
+        make_identity(nc, ident_f32[:])
+        ident_bf = keep.tile([P, P], BF16)
+        make_identity(nc, ident_bf[:])
+
+        mask_bf = keep.tile([P, TILES], BF16)
+        nc.scalar.dma_start(out=mask_bf[:], in_=mask.rearrange("(p j) -> p j", j=TILES))
+        mask_f32 = keep.tile([P, TILES], F32)
+        nc.gpsimd.tensor_copy(out=mask_f32[:], in_=mask_bf[:])
+
         w_small = keep.tile([P, N_ALL], BF16)
+        w_small_ps = plain_banks.tile([P, 7, D_H], BF16, tag="plain")
+        for b in range(7):
+            nc.tensor.transpose(w_small_ps[:, b, :], w_small_rows[:, b, :], ident_bf[:])
+        nc.scalar.copy(out=w_small[:], in_=w_small_ps[:].rearrange("k b c -> k (b c)"))
+
         bias_cell = keep.tile([P, N_CELL], F32)
-        with tc.psum_pool(name="setup_psum", bufs=1) as setup_psum:
-            w_small_ps = setup_psum.tile([P, 7, D_H], BF16)
-            for b in range(7):
-                nc.tensor.transpose(w_small_ps[:, b, :], w_small_rows[:, b, :], ident_bf[:])
-            nc.scalar.copy(out=w_small[:], in_=w_small_ps[:].rearrange("k b c -> k (b c)"))
-            bias_cell_ps = setup_psum.tile([P, N_CELL], F32)
+
+        def spread_bias():
+            bias_cell_ps = plain_banks.tile([P, N_CELL], F32, tag="plain")
             nc.tensor.matmul(bias_cell_ps[:], lhsT=ones[:], rhs=bias_rows[:, 0:N_CELL], start=True, stop=True)
             nc.vector.tensor_copy(out=bias_cell[:], in_=bias_cell_ps[:])
 
-        side = [keep.tile([P, TILES, D_H], BF16, name="side%d" % w) for w in range(5)]
-
-        x_pool = ctx.enter_context(tc.tile_pool(name="x_pool", bufs=4))
-        stage = ctx.enter_context(tc.tile_pool(name="stage", bufs=4))
-        work = ctx.enter_context(tc.tile_pool(name="work", bufs=3))
-        pre_pool = ctx.enter_context(tc.tile_pool(name="pre_pool", bufs=2))
-        late = ctx.enter_context(tc.tile_pool(name="late", bufs=4))
-        psum1 = ctx.enter_context(tc.psum_pool(name="psum1", bufs=1))
-        psum2 = ctx.enter_context(tc.psum_pool(name="psum2", bufs=2))
-
-        x_of = {}
-        hst_of = {}
-        grouped_of = {}
-        codes_of = {}
-        scales_of = {}
-        lin_of = {}
-        pre_of = {}
-        gates_of = {}
-        diff_of = {}
-        tc_of = {}
-
-        def load(k):
-            if (2 * k) % SIDE_CHUNK == 0:
-                rows = slice(2 * k, 2 * k + SIDE_CHUNK)
-                for w in range(5):
-                    nc.sync.dma_start(out=side[w][:, rows, :], in_=side_rows[w][:, rows, :])
-            x_sb = x_pool.tile([P, 2, D_IN], BF16)
-            nc.sync.dma_start(out=x_sb[:], in_=x_rows[:, 2 * k : 2 * k + 2, :])
-            x_of[k] = x_sb
-
         def front(k):
-            hst_ps = psum1.tile([P, 2, 4, P], BF16)
+            hst_ps = plain_banks.tile([P, 2, 4, P], BF16, tag="plain")
             for jj in range(2):
                 for w in range(4):
                     nc.tensor.transpose(hst_ps[:, jj, w, :], side[w][:, 2 * k + jj, :], ident_bf[:])
@@ -156,7 +160,7 @@ def tile_share_lstm_cell_pa_t_kernel(
             grouped = stage.tile([P, 2, PASSES, P, 4], BF16, align_bytes=64)
             for jj in range(2):
                 x_words = x_of[k][:, jj, :].bitcast(F32)
-                xt_ps = psum2.tile([P, PASSES, 2, P], F32)
+                xt_ps = plain_banks.tile([P, PASSES, 2, P], F32, tag="plain")
                 for g in range(PASSES):
                     for u in range(2):
                         nc.tensor.transpose(
@@ -180,22 +184,26 @@ def tile_share_lstm_cell_pa_t_kernel(
                 in_=grouped_of[k][:, jj].rearrange("p g r t -> p (g r t)"),
             )
 
-        def small_products(k, jj):
-            if jj == 0:
-                lin = work.tile([P, 2, N_ALL], F32)
-                lin_of[k] = lin
-            lin = lin_of[k]
+        def small_products(k):
+            lin = work.tile([P, 2, N_ALL], F32)
+            lin_of[k] = lin
             hst = hst_of[k]
-            cell_ps = psum1.tile([P, N_CELL], F32)
-            nc.tensor.matmul(cell_ps[:], lhsT=hst[:, jj, 0, :], rhs=w_small[:, 0:N_CELL], start=True, stop=True)
-            share_ps = psum1.tile([P, N_SHARE], F32)
-            for b in range(3):
-                cols = slice(N_CELL + D_H * b, N_CELL + D_H * (b + 1))
-                acc = share_ps[:, D_H * b : D_H * (b + 1)]
-                nc.tensor.matmul(acc, lhsT=ones[:], rhs=bias_rows[:, cols], start=True, stop=False)
-                nc.tensor.matmul(acc, lhsT=hst[:, jj, 1 + b, :], rhs=w_small[:, cols], start=False, stop=True)
-            nc.vector.tensor_tensor(out=lin[:, jj, 0:N_CELL], in0=cell_ps[:], in1=bias_cell[:], op=ALU.add)
-            nc.scalar.copy(out=lin[:, jj, N_CELL:N_ALL], in_=share_ps[:])
+            for jj in range(2):
+                cell_ps = plain_banks.tile([P, N_CELL], F32, tag="plain")
+                nc.tensor.matmul(cell_ps[:], lhsT=hst[:, jj, 0, :], rhs=w_small[:, 0:N_CELL], start=True, stop=True)
+                cell_ps_of[(k, jj)] = cell_ps
+                share_ps = plain_banks.tile([P, N_SHARE], F32, tag="plain")
+                for b in range(3):
+                    cols = slice(N_CELL + D_H * b, N_CELL + D_H * (b + 1))
+                    acc = share_ps[:, D_H * b : D_H * (b + 1)]
+                    nc.tensor.matmul(acc, lhsT=ones[:], rhs=bias_rows[:, cols], start=True, stop=False)
+                    nc.tensor.matmul(acc, lhsT=hst[:, jj, 1 + b, :], rhs=w_small[:, cols], start=False, stop=True)
+                nc.scalar.copy(out=lin[:, jj, N_CELL:N_ALL], in_=share_ps[:])
+
+        def cell_bias(k, jj):
+            nc.vector.tensor_tensor(
+                out=lin_of[k][:, jj, 0:N_CELL], in0=cell_ps_of[(k, jj)][:], in1=bias_cell[:], op=ALU.add
+            )
 
         def mx_group(acc, k, jj, first, width):
             for g in range(PASSES):
@@ -209,66 +217,74 @@ def tile_share_lstm_cell_pa_t_kernel(
                     stop=(g == PASSES - 1),
                 )
 
-        def big_product(k, jj):
-            if jj == 0:
-                pre = pre_pool.tile([P, 2, N_ALL], F32)
-                gates = late.tile([P, 2, N_ALL], F32)
-                pre_of[k] = pre
-                gates_of[k] = gates
-            pre = pre_of[k]
-            gates = gates_of[k]
+        def big_product(k):
+            for jj in range(2):
+                mx_cell_ps = mx_banks.tile([P, N_CELL], F32, tag="mx")
+                mx_group(mx_cell_ps[:], k, jj, 0, N_CELL)
+                mx_share_ps = mx_banks.tile([P, N_SHARE], F32, tag="mx")
+                for b in range(3):
+                    mx_group(mx_share_ps[:, D_H * b : D_H * (b + 1)], k, jj, N_CELL + D_H * b, D_H)
+                mx_ps_of[(k, jj)] = (mx_cell_ps, mx_share_ps)
+
+        def activate(k):
+            pre = pre_pool.tile([P, 2, N_ALL], F32)
+            gates = work.tile([P, 2, N_ALL], F32)
+            gates_of[k] = gates
             lin = lin_of[k]
-            mx_cell_ps = psum2.tile([P, N_CELL], F32)
-            mx_group(mx_cell_ps[:], k, jj, 0, N_CELL)
-            mx_share_ps = psum1.tile([P, N_SHARE], F32)
+            for jj in range(2):
+                mx_cell_ps, mx_share_ps = mx_ps_of[(k, jj)]
+                nc.vector.tensor_tensor(out=pre[:, jj, 0:N_CELL], in0=mx_cell_ps[:], in1=lin[:, jj, 0:N_CELL], op=ALU.add)
+                nc.vector.tensor_tensor(
+                    out=pre[:, jj, N_CELL:N_ALL], in0=mx_share_ps[:], in1=lin[:, jj, N_CELL:N_ALL], op=ALU.add
+                )
+                nc.scalar.activation(out=gates[:, jj, 0 : 3 * D_H], in_=pre[:, jj, 0 : 3 * D_H], func=ACT.Sigmoid)
+                nc.scalar.activation(out=gates[:, jj, 3 * D_H : N_CELL], in_=pre[:, jj, 3 * D_H : N_CELL], func=ACT.Tanh)
+                nc.scalar.activation(out=gates[:, jj, N_CELL:N_ALL], in_=pre[:, jj, N_CELL:N_ALL], func=ACT.Sigmoid)
+
+        def gate_of(k, b):
+            return gates_of[k][:, :, D_H * b : D_H * (b + 1)]
+
+        def differences(k):
+            diff = work.tile([P, 3, 2, D_H], F32)
             for b in range(3):
-                mx_group(mx_share_ps[:, D_H * b : D_H * (b + 1)], k, jj, N_CELL + D_H * b, D_H)
-            nc.vector.tensor_tensor(out=pre[:, jj, 0:N_CELL], in0=mx_cell_ps[:], in1=lin[:, jj, 0:N_CELL], op=ALU.add)
-            nc.vector.tensor_tensor(
-                out=pre[:, jj, N_CELL:N_ALL], in0=mx_share_ps[:], in1=lin[:, jj, N_CELL:N_ALL], op=ALU.add
-            )
-            nc.scalar.activation(out=gates[:, jj, 0 : 3 * D_H], in_=pre[:, jj, 0 : 3 * D_H], func=ACT.Sigmoid)
-            nc.scalar.activation(out=gates[:, jj, 3 * D_H : N_CELL], in_=pre[:, jj, 3 * D_H : N_CELL], func=ACT.Tanh)
-            nc.scalar.activation(out=gates[:, jj, N_CELL:N_ALL], in_=pre[:, jj, N_CELL:N_ALL], func=ACT.Sigmoid)
+                nc.gpsimd.tensor_tensor(out=diff[:, b], in0=gate_of(k, 4 + b), in1=gate_of(k, 2), op=ALU.subtract)
+            diff_of[k] = diff
 
         def cell(k):
-            gates = gates_of[k]
-            gate = [gates[:, :, D_H * b : D_H * (b + 1)] for b in range(7)]
-            in_part = work.tile([P, 2, D_H], F32)
-            nc.gpsimd.tensor_tensor(out=in_part[:], in0=gate[0], in1=gate[3], op=ALU.mult)
             keep_part = work.tile([P, 2, D_H], F32)
-            nc.gpsimd.tensor_tensor(out=keep_part[:], in0=gate[1], in1=side[4][:, 2 * k : 2 * k + 2, :], op=ALU.mult)
+            nc.vector.tensor_tensor(out=keep_part[:], in0=gate_of(k, 1), in1=side[4][:, 2 * k : 2 * k + 2, :], op=ALU.mult)
+            in_part = work.tile([P, 2, D_H], F32)
+            nc.vector.tensor_tensor(out=in_part[:], in0=gate_of(k, 0), in1=gate_of(k, 3), op=ALU.mult)
+            if k + 1 < PAIRS:
+                cell_bias(k + 1, 0)
             c_raw = work.tile([P, 2, D_H], F32)
-            nc.gpsimd.tensor_tensor(out=c_raw[:], in0=in_part[:], in1=keep_part[:], op=ALU.add)
-            diff = late.tile([P, 3, 2, D_H], F32)
-            for b in range(3):
-                nc.gpsimd.tensor_tensor(out=diff[:, b], in0=gate[4 + b], in1=gate[2], op=ALU.subtract)
-            diff_of[k] = diff
-            c_t = late.tile([P, 2, D_H], F32)
+            nc.vector.tensor_tensor(out=c_raw[:], in0=in_part[:], in1=keep_part[:], op=ALU.add)
+            if k + 1 < PAIRS:
+                cell_bias(k + 1, 1)
+            c_t = work.tile([P, 2, D_H], F32)
             tanh_c = work.tile([P, 2, D_H], F32)
-            tc_m = late.tile([P, 2, D_H], F32)
+            tc_m = work.tile([P, 2, D_H], F32)
             for jj in range(2):
                 m = mask_f32[:, 2 * k + jj : 2 * k + jj + 1]
                 nc.scalar.activation(out=tanh_c[:, jj, :], in_=c_raw[:, jj, :], func=ACT.Tanh, scale=m)
-                nc.scalar.activation(out=c_t[:, jj, :], in_=c_raw[:, jj, :], func=ACT.Copy, scale=m)
                 nc.scalar.activation(out=tc_m[:, jj, :], in_=tanh_c[:, jj, :], func=ACT.Copy, scale=m)
+                nc.scalar.activation(out=c_t[:, jj, :], in_=c_raw[:, jj, :], func=ACT.Copy, scale=m)
             nc.sync.dma_start(out=out_rows[1][:, 2 * k : 2 * k + 2, :], in_=c_t[:])
             tc_of[k] = tc_m
 
         def tail(k, next_k):
-            o_gate = gates_of[k][:, :, 2 * D_H : 3 * D_H]
             diff = diff_of[k]
             tc_m = tc_of[k]
             rows = slice(2 * k, 2 * k + 2)
-            s_0 = late.tile([P, 2, D_H], F32)
+            s_0 = work.tile([P, 2, D_H], F32)
             nc.vector.scalar_tensor_tensor(out=s_0[:], in0=diff[:, 0], scalar=1.0, in1=tc_m[:], op0=ALU.add, op1=ALU.mult)
-            h_t = late.tile([P, 2, D_H], F32)
-            nc.vector.tensor_tensor(out=h_t[:], in0=o_gate, in1=tc_m[:], op=ALU.mult)
+            h_t = work.tile([P, 2, D_H], F32)
+            nc.vector.tensor_tensor(out=h_t[:], in0=gate_of(k, 2), in1=tc_m[:], op=ALU.mult)
             rest_1 = work.tile([P, 2, D_H], F32)
             nc.vector.scalar_tensor_tensor(out=rest_1[:], in0=diff[:, 1], scalar=2.0, in1=s_0[:], op0=ALU.add, op1=ALU.subtract)
             rest_2 = work.tile([P, 2, D_H], F32)
             nc.vector.scalar_tensor_tensor(out=rest_2[:], in0=s_0[:], scalar=-2.0, in1=diff[:, 2], op0=ALU.mult, op1=ALU.add)
-            s_1 = late.tile([P, 2, D_H], F32)
+            s_1 = work.tile([P, 2, D_H], F32)
             nc.vector.scalar_tensor_tensor(out=s_1[:], in0=rest_1[:], scalar=0.5, in1=tc_m[:], op0=ALU.mult, op1=ALU.mult)
             if next_k < PAIRS:
                 quantise(next_k, 0)
@@ -276,40 +292,35 @@ def tile_share_lstm_cell_pa_t_kernel(
             nc.vector.scalar_tensor_tensor(out=rest_3[:], in0=rest_2[:], scalar=3.0, in1=s_1[:], op0=ALU.add, op1=ALU.subtract)
             if next_k < PAIRS:
                 quantise(next_k, 1)
-            s_2 = late.tile([P, 2, D_H], F32)
+            s_2 = work.tile([P, 2, D_H], F32)
             nc.vector.scalar_tensor_tensor(out=s_2[:], in0=rest_3[:], scalar=1.0 / 3.0, in1=tc_m[:], op0=ALU.mult, op1=ALU.mult)
             nc.sync.dma_start(out=out_rows[0][:, rows, :], in_=h_t[:])
             nc.sync.dma_start(out=out_rows[2][:, rows, :], in_=s_0[:])
             nc.sync.dma_start(out=out_rows[3][:, rows, :], in_=s_1[:])
             nc.sync.dma_start(out=out_rows[4][:, rows, :], in_=s_2[:])
 
-        ctx.enter_context(tc.manual_schedule())
-        for k in range(4):
-            load(k)
-        for k in range(3):
-            front(k)
-        for k in range(2):
-            new_codes(k)
-            quantise(k, 0)
-            quantise(k, 1)
-        small_products(0, 0)
-        small_products(0, 1)
-        for n in range(PAIRS + 2):
-            if n + 4 < PAIRS:
+        for n in range(-4, PAIRS + 1):
+            if 1 <= n + 4 < PAIRS:
                 load(n + 4)
-            for jj in range(2):
-                if n + 1 < PAIRS:
-                    small_products(n + 1, jj)
-                if n < PAIRS:
-                    big_product(n, jj)
-            if n + 3 < PAIRS:
+            if 0 <= n < PAIRS:
+                big_product(n)
+                activate(n)
+            if 0 <= n + 3 < PAIRS:
                 front(n + 3)
-            if n + 2 < PAIRS:
+            if 0 <= n + 2 < PAIRS:
                 new_codes(n + 2)
-            if 1 <= n <= PAIRS:
-                cell(n - 1)
-            if n >= 2:
-                tail(n - 2, n + 2)
-            elif n + 2 < PAIRS:
+            if n + 1 == 0:
+                spread_bias()
+            if 0 <= n + 1 < PAIRS:
+                small_products(n + 1)
+            if n + 1 == 0:
+                cell_bias(0, 0)
+                cell_bias(0, 1)
+            if 0 <= n - 1:
+                differences(n - 1)
+                tail(n - 1, n + 2)
+            elif 0 <= n + 2:
                 quantise(n + 2, 0)
                 quantise(n + 2, 1)
+            if 0 <= n < PAIRS:
+                cell(n)

@@ -171,18 +171,16 @@ def tile_share_lstm_cell_pa_t_kernel(
                 )
             grouped_of[k] = grouped
 
-        def new_codes(k):
+        def quantise(k):
             codes = work.tile([P, 2, PASSES, P], U32, align_bytes=64)
             scales = work.tile([P, 2, PASSES, P], U8, align_bytes=64)
+            nc.vector.quantize_mx(
+                out=codes[:].rearrange("p j g r -> p (j g r)").bitcast(FP8X4),
+                scales=scales[:].rearrange("p j g r -> p (j g r)"),
+                in_=grouped_of[k][:].rearrange("p j g r t -> p (j g r t)"),
+            )
             codes_of[k] = codes
             scales_of[k] = scales
-
-        def quantise(k, jj):
-            nc.vector.quantize_mx(
-                out=codes_of[k][:, jj].rearrange("p g r -> p (g r)").bitcast(FP8X4),
-                scales=scales_of[k][:, jj].rearrange("p g r -> p (g r)"),
-                in_=grouped_of[k][:, jj].rearrange("p g r t -> p (g r t)"),
-            )
 
         def small_products(k):
             lin = work.tile([P, 2, N_ALL], F32)
@@ -250,77 +248,74 @@ def tile_share_lstm_cell_pa_t_kernel(
                 nc.gpsimd.tensor_tensor(out=diff[:, b], in0=gate_of(k, 4 + b), in1=gate_of(k, 2), op=ALU.subtract)
             diff_of[k] = diff
 
-        def cell(k):
-            keep_part = work.tile([P, 2, D_H], F32)
-            nc.vector.tensor_tensor(out=keep_part[:], in0=gate_of(k, 1), in1=side[4][:, 2 * k : 2 * k + 2, :], op=ALU.mult)
-            in_part = work.tile([P, 2, D_H], F32)
-            nc.vector.tensor_tensor(out=in_part[:], in0=gate_of(k, 0), in1=gate_of(k, 3), op=ALU.mult)
-            if k + 1 < PAIRS:
-                cell_bias(k + 1, 0)
-            c_raw = work.tile([P, 2, D_H], F32)
-            nc.vector.tensor_tensor(out=c_raw[:], in0=in_part[:], in1=keep_part[:], op=ALU.add)
-            if k + 1 < PAIRS:
-                cell_bias(k + 1, 1)
-            c_t = work.tile([P, 2, D_H], F32)
-            tanh_c = work.tile([P, 2, D_H], F32)
-            tc_m = work.tile([P, 2, D_H], F32)
-            for jj in range(2):
-                m = mask_f32[:, 2 * k + jj : 2 * k + jj + 1]
-                nc.scalar.activation(out=tanh_c[:, jj, :], in_=c_raw[:, jj, :], func=ACT.Tanh, scale=m)
-                nc.scalar.activation(out=tc_m[:, jj, :], in_=tanh_c[:, jj, :], func=ACT.Copy, scale=m)
-                nc.scalar.activation(out=c_t[:, jj, :], in_=c_raw[:, jj, :], func=ACT.Copy, scale=m)
-            nc.sync.dma_start(out=out_rows[1][:, 2 * k : 2 * k + 2, :], in_=c_t[:])
-            tc_of[k] = tc_m
-
-        def tail(k, next_k):
-            diff = diff_of[k]
-            tc_m = tc_of[k]
-            rows = slice(2 * k, 2 * k + 2)
-            s_0 = work.tile([P, 2, D_H], F32)
-            nc.vector.scalar_tensor_tensor(out=s_0[:], in0=diff[:, 0], scalar=1.0, in1=tc_m[:], op0=ALU.add, op1=ALU.mult)
+        def hidden(k):
             h_t = work.tile([P, 2, D_H], F32)
-            nc.vector.tensor_tensor(out=h_t[:], in0=gate_of(k, 2), in1=tc_m[:], op=ALU.mult)
-            rest_1 = work.tile([P, 2, D_H], F32)
-            nc.vector.scalar_tensor_tensor(out=rest_1[:], in0=diff[:, 1], scalar=2.0, in1=s_0[:], op0=ALU.add, op1=ALU.subtract)
-            rest_2 = work.tile([P, 2, D_H], F32)
-            nc.vector.scalar_tensor_tensor(out=rest_2[:], in0=s_0[:], scalar=-2.0, in1=diff[:, 2], op0=ALU.mult, op1=ALU.add)
-            s_1 = work.tile([P, 2, D_H], F32)
-            nc.vector.scalar_tensor_tensor(out=s_1[:], in0=rest_1[:], scalar=0.5, in1=tc_m[:], op0=ALU.mult, op1=ALU.mult)
-            if next_k < PAIRS:
-                quantise(next_k, 0)
-            rest_3 = work.tile([P, 2, D_H], F32)
-            nc.vector.scalar_tensor_tensor(out=rest_3[:], in0=rest_2[:], scalar=3.0, in1=s_1[:], op0=ALU.add, op1=ALU.subtract)
-            if next_k < PAIRS:
-                quantise(next_k, 1)
-            s_2 = work.tile([P, 2, D_H], F32)
-            nc.vector.scalar_tensor_tensor(out=s_2[:], in0=rest_3[:], scalar=1.0 / 3.0, in1=tc_m[:], op0=ALU.mult, op1=ALU.mult)
-            nc.sync.dma_start(out=out_rows[0][:, rows, :], in_=h_t[:])
-            nc.sync.dma_start(out=out_rows[2][:, rows, :], in_=s_0[:])
-            nc.sync.dma_start(out=out_rows[3][:, rows, :], in_=s_1[:])
-            nc.sync.dma_start(out=out_rows[4][:, rows, :], in_=s_2[:])
+            nc.gpsimd.tensor_tensor(out=h_t[:], in0=gate_of(k, 2), in1=tc_of[k][:], op=ALU.mult)
+            nc.sync.dma_start(out=out_rows[0][:, 2 * k : 2 * k + 2, :], in_=h_t[:])
 
-        for n in range(-4, PAIRS + 1):
-            if 1 <= n + 4 < PAIRS:
-                load(n + 4)
+        def finish(done, k):
+            if 0 <= done:
+                diff = diff_of[done]
+                tc_m = tc_of[done]
+                s_0 = work.tile([P, 2, D_H], F32)
+                nc.vector.scalar_tensor_tensor(out=s_0[:], in0=diff[:, 0], scalar=1.0, in1=tc_m[:], op0=ALU.add, op1=ALU.mult)
+            if k < PAIRS:
+                keep_part = work.tile([P, 2, D_H], F32)
+                nc.vector.tensor_tensor(out=keep_part[:], in0=gate_of(k, 1), in1=side[4][:, 2 * k : 2 * k + 2, :], op=ALU.mult)
+            if 0 <= done:
+                rest_1 = work.tile([P, 2, D_H], F32)
+                nc.vector.scalar_tensor_tensor(out=rest_1[:], in0=diff[:, 1], scalar=2.0, in1=s_0[:], op0=ALU.add, op1=ALU.subtract)
+                rest_2 = work.tile([P, 2, D_H], F32)
+                nc.vector.scalar_tensor_tensor(out=rest_2[:], in0=s_0[:], scalar=-2.0, in1=diff[:, 2], op0=ALU.mult, op1=ALU.add)
+                s_1 = work.tile([P, 2, D_H], F32)
+                nc.vector.scalar_tensor_tensor(out=s_1[:], in0=rest_1[:], scalar=0.5, in1=tc_m[:], op0=ALU.mult, op1=ALU.mult)
+            if k < PAIRS:
+                in_part = work.tile([P, 2, D_H], F32)
+                nc.vector.tensor_tensor(out=in_part[:], in0=gate_of(k, 0), in1=gate_of(k, 3), op=ALU.mult)
+            if 0 <= done:
+                rest_3 = work.tile([P, 2, D_H], F32)
+                nc.vector.scalar_tensor_tensor(out=rest_3[:], in0=rest_2[:], scalar=3.0, in1=s_1[:], op0=ALU.add, op1=ALU.subtract)
+            if k < PAIRS:
+                c_raw = work.tile([P, 2, D_H], F32)
+                nc.vector.tensor_tensor(out=c_raw[:], in0=in_part[:], in1=keep_part[:], op=ALU.add)
+            if 0 <= done:
+                s_2 = work.tile([P, 2, D_H], F32)
+                nc.vector.scalar_tensor_tensor(out=s_2[:], in0=rest_3[:], scalar=1.0 / 3.0, in1=tc_m[:], op0=ALU.mult, op1=ALU.mult)
+                rows = slice(2 * done, 2 * done + 2)
+                nc.sync.dma_start(out=out_rows[2][:, rows, :], in_=s_0[:])
+                nc.sync.dma_start(out=out_rows[3][:, rows, :], in_=s_1[:])
+                nc.sync.dma_start(out=out_rows[4][:, rows, :], in_=s_2[:])
+            if k < PAIRS:
+                c_t = work.tile([P, 2, D_H], F32)
+                tanh_c = work.tile([P, 2, D_H], F32)
+                tc_m = work.tile([P, 2, D_H], F32)
+                for jj in range(2):
+                    m = mask_f32[:, 2 * k + jj : 2 * k + jj + 1]
+                    nc.scalar.activation(out=tanh_c[:, jj, :], in_=c_raw[:, jj, :], func=ACT.Tanh, scale=m)
+                    nc.scalar.activation(out=tc_m[:, jj, :], in_=tanh_c[:, jj, :], func=ACT.Copy, scale=m)
+                    nc.scalar.activation(out=c_t[:, jj, :], in_=c_raw[:, jj, :], func=ACT.Copy, scale=m)
+                nc.sync.dma_start(out=out_rows[1][:, 2 * k : 2 * k + 2, :], in_=c_t[:])
+                tc_of[k] = tc_m
+
+        for n in range(-3, PAIRS + 1):
+            if 1 <= n + 3 < PAIRS:
+                load(n + 3)
             if 0 <= n < PAIRS:
                 big_product(n)
+            if 0 <= n + 1 < PAIRS:
+                small_products(n + 1)
+            if 0 <= n < PAIRS:
                 activate(n)
-            if 0 <= n + 3 < PAIRS:
-                front(n + 3)
-            if 0 <= n + 2 < PAIRS:
-                new_codes(n + 2)
+                differences(n)
             if n + 1 == 0:
                 spread_bias()
             if 0 <= n + 1 < PAIRS:
-                small_products(n + 1)
-            if n + 1 == 0:
-                cell_bias(0, 0)
-                cell_bias(0, 1)
+                cell_bias(n + 1, 0)
+                cell_bias(n + 1, 1)
+                quantise(n + 1)
+            if 0 <= n + 2 < PAIRS:
+                front(n + 2)
             if 0 <= n - 1:
-                differences(n - 1)
-                tail(n - 1, n + 2)
-            elif 0 <= n + 2:
-                quantise(n + 2, 0)
-                quantise(n + 2, 1)
-            if 0 <= n < PAIRS:
-                cell(n)
+                hidden(n - 1)
+            if 0 <= n:
+                finish(n - 1, n)

@@ -99,6 +99,16 @@ def tile_share_lstm_cell_pa_t_kernel(
             nc.scalar.dma_start(out=w_small_rows[:, 4 + b, :], in_=w_sh)
 
         load(0)
+        load(1)
+
+        bias_rows = keep.tile([P, N_ALL], BF16)
+        nc.vector.memset(bias_rows[:], 0.0)
+        nc.scalar.dma_start(out=bias_rows[0:1, :], in_=bias_ih.unsqueeze(0))
+        nc.scalar.dma_start(out=bias_rows[1:2, 0:N_CELL], in_=bias_hh.unsqueeze(0))
+        for b, b_sh in enumerate((bias_sh0, bias_sh1, bias_sh2)):
+            nc.scalar.dma_start(
+                out=bias_rows[1:2, N_CELL + D_H * b : N_CELL + D_H * (b + 1)], in_=b_sh.unsqueeze(0)
+            )
 
         w_words = keep.tile([P, PASSES, 2 * N_ALL], U8, align_bytes=64)
         nc.sync.dma_start(
@@ -115,14 +125,6 @@ def tile_share_lstm_cell_pa_t_kernel(
                 .bitcast(I32),
             )
 
-        bias_rows = keep.tile([P, N_ALL], BF16)
-        nc.vector.memset(bias_rows[:], 0.0)
-        nc.scalar.dma_start(out=bias_rows[0:1, :], in_=bias_ih.unsqueeze(0))
-        nc.scalar.dma_start(out=bias_rows[1:2, 0:N_CELL], in_=bias_hh.unsqueeze(0))
-        for b, b_sh in enumerate((bias_sh0, bias_sh1, bias_sh2)):
-            nc.scalar.dma_start(
-                out=bias_rows[1:2, N_CELL + D_H * b : N_CELL + D_H * (b + 1)], in_=b_sh.unsqueeze(0)
-            )
         ones = keep.tile([P, P], BF16)
         nc.vector.memset(ones[:], 1.0)
 
@@ -150,13 +152,6 @@ def tile_share_lstm_cell_pa_t_kernel(
             nc.vector.tensor_copy(out=bias_cell[:], in_=bias_cell_ps[:])
 
         def front(k):
-            hst_ps = plain_banks.tile([P, 2, 4, P], BF16, tag="plain")
-            for jj in range(2):
-                for w in range(4):
-                    nc.tensor.transpose(hst_ps[:, jj, w, :], side[w][:, 2 * k + jj, :], ident_bf[:])
-            hst = stage.tile([P, 2, 4, P], BF16)
-            nc.scalar.copy(out=hst[:], in_=hst_ps[:])
-            hst_of[k] = hst
             grouped = stage.tile([P, 2, PASSES, P, 4], BF16, align_bytes=64)
             for jj in range(2):
                 x_words = x_of[k][:, jj, :].bitcast(F32)
@@ -170,6 +165,13 @@ def tile_share_lstm_cell_pa_t_kernel(
                     out=grouped[:, jj].bitcast(F32), in_=xt_ps[:].rearrange("p g u r -> p g r u")
                 )
             grouped_of[k] = grouped
+            hst_ps = plain_banks.tile([P, 2, 4, P], BF16, tag="plain")
+            for jj in range(2):
+                for w in range(4):
+                    nc.tensor.transpose(hst_ps[:, jj, w, :], side[w][:, 2 * k + jj, :], ident_bf[:])
+            hst = stage.tile([P, 2, 4, P], BF16)
+            nc.scalar.copy(out=hst[:], in_=hst_ps[:])
+            hst_of[k] = hst
 
         def quantise(k):
             codes = work.tile([P, 2, PASSES, P], U32, align_bytes=64)
@@ -243,9 +245,13 @@ def tile_share_lstm_cell_pa_t_kernel(
             return gates_of[k][:, :, D_H * b : D_H * (b + 1)]
 
         def differences(k):
-            diff = work.tile([P, 3, 2, D_H], F32)
-            for b in range(3):
-                nc.gpsimd.tensor_tensor(out=diff[:, b], in0=gate_of(k, 4 + b), in1=gate_of(k, 2), op=ALU.subtract)
+            diff = work.tile([P, 2, 3, D_H], F32)
+            nc.gpsimd.tensor_tensor(
+                out=diff[:],
+                in0=gates_of[k][:, :, N_CELL:N_ALL].rearrange("p j (b d) -> p j b d", b=3),
+                in1=gate_of(k, 2).unsqueeze(2).to_broadcast([P, 2, 3, D_H]),
+                op=ALU.subtract,
+            )
             diff_of[k] = diff
 
         def hidden(k):
@@ -258,15 +264,15 @@ def tile_share_lstm_cell_pa_t_kernel(
                 diff = diff_of[done]
                 tc_m = tc_of[done]
                 s_0 = work.tile([P, 2, D_H], F32)
-                nc.vector.scalar_tensor_tensor(out=s_0[:], in0=diff[:, 0], scalar=1.0, in1=tc_m[:], op0=ALU.add, op1=ALU.mult)
+                nc.vector.scalar_tensor_tensor(out=s_0[:], in0=diff[:, :, 0, :], scalar=1.0, in1=tc_m[:], op0=ALU.add, op1=ALU.mult)
             if k < PAIRS:
                 keep_part = work.tile([P, 2, D_H], F32)
                 nc.vector.tensor_tensor(out=keep_part[:], in0=gate_of(k, 1), in1=side[4][:, 2 * k : 2 * k + 2, :], op=ALU.mult)
             if 0 <= done:
                 rest_1 = work.tile([P, 2, D_H], F32)
-                nc.vector.scalar_tensor_tensor(out=rest_1[:], in0=diff[:, 1], scalar=2.0, in1=s_0[:], op0=ALU.add, op1=ALU.subtract)
+                nc.vector.scalar_tensor_tensor(out=rest_1[:], in0=diff[:, :, 1, :], scalar=2.0, in1=s_0[:], op0=ALU.add, op1=ALU.subtract)
                 rest_2 = work.tile([P, 2, D_H], F32)
-                nc.vector.scalar_tensor_tensor(out=rest_2[:], in0=s_0[:], scalar=-2.0, in1=diff[:, 2], op0=ALU.mult, op1=ALU.add)
+                nc.vector.scalar_tensor_tensor(out=rest_2[:], in0=s_0[:], scalar=-2.0, in1=diff[:, :, 2, :], op0=ALU.mult, op1=ALU.add)
                 s_1 = work.tile([P, 2, D_H], F32)
                 nc.vector.scalar_tensor_tensor(out=s_1[:], in0=rest_1[:], scalar=0.5, in1=tc_m[:], op0=ALU.mult, op1=ALU.mult)
             if k < PAIRS:
@@ -298,7 +304,7 @@ def tile_share_lstm_cell_pa_t_kernel(
                 tc_of[k] = tc_m
 
         for n in range(-3, PAIRS + 1):
-            if 1 <= n + 3 < PAIRS:
+            if 2 <= n + 3 < PAIRS:
                 load(n + 3)
             if 0 <= n < PAIRS:
                 big_product(n)

@@ -61,7 +61,6 @@ def tile_share_lstm_cell_pa_t_kernel(
     out_rows = [a.rearrange("(p j) d -> p j d", j=TILES) for a in (out_0, out_1, out_2, out_3, out_4)]
 
     with ExitStack() as ctx:
-        ctx.enter_context(tc.manual_schedule())
         keep = ctx.enter_context(tc.tile_pool(name="keep", bufs=1))
         x_pool = ctx.enter_context(tc.tile_pool(name="x_pool", bufs=4))
         stage = ctx.enter_context(tc.tile_pool(name="stage", bufs=4))
@@ -99,16 +98,6 @@ def tile_share_lstm_cell_pa_t_kernel(
             nc.scalar.dma_start(out=w_small_rows[:, 4 + b, :], in_=w_sh)
 
         load(0)
-        load(1)
-
-        bias_rows = keep.tile([P, N_ALL], BF16)
-        nc.vector.memset(bias_rows[:], 0.0)
-        nc.scalar.dma_start(out=bias_rows[0:1, :], in_=bias_ih.unsqueeze(0))
-        nc.scalar.dma_start(out=bias_rows[1:2, 0:N_CELL], in_=bias_hh.unsqueeze(0))
-        for b, b_sh in enumerate((bias_sh0, bias_sh1, bias_sh2)):
-            nc.scalar.dma_start(
-                out=bias_rows[1:2, N_CELL + D_H * b : N_CELL + D_H * (b + 1)], in_=b_sh.unsqueeze(0)
-            )
 
         w_words = keep.tile([P, PASSES, 2 * N_ALL], U8, align_bytes=64)
         nc.sync.dma_start(
@@ -125,6 +114,14 @@ def tile_share_lstm_cell_pa_t_kernel(
                 .bitcast(I32),
             )
 
+        bias_rows = keep.tile([P, N_ALL], BF16)
+        nc.vector.memset(bias_rows[:], 0.0)
+        nc.scalar.dma_start(out=bias_rows[0:1, :], in_=bias_ih.unsqueeze(0))
+        nc.scalar.dma_start(out=bias_rows[1:2, 0:N_CELL], in_=bias_hh.unsqueeze(0))
+        for b, b_sh in enumerate((bias_sh0, bias_sh1, bias_sh2)):
+            nc.scalar.dma_start(
+                out=bias_rows[1:2, N_CELL + D_H * b : N_CELL + D_H * (b + 1)], in_=b_sh.unsqueeze(0)
+            )
         ones = keep.tile([P, P], BF16)
         nc.vector.memset(ones[:], 1.0)
 
@@ -152,6 +149,13 @@ def tile_share_lstm_cell_pa_t_kernel(
             nc.vector.tensor_copy(out=bias_cell[:], in_=bias_cell_ps[:])
 
         def front(k):
+            hst_ps = plain_banks.tile([P, 2, 4, P], BF16, tag="plain")
+            for jj in range(2):
+                for w in range(4):
+                    nc.tensor.transpose(hst_ps[:, jj, w, :], side[w][:, 2 * k + jj, :], ident_bf[:])
+            hst = stage.tile([P, 2, 4, P], BF16)
+            nc.scalar.copy(out=hst[:], in_=hst_ps[:])
+            hst_of[k] = hst
             grouped = stage.tile([P, 2, PASSES, P, 4], BF16, align_bytes=64)
             for jj in range(2):
                 x_words = x_of[k][:, jj, :].bitcast(F32)
@@ -165,13 +169,6 @@ def tile_share_lstm_cell_pa_t_kernel(
                     out=grouped[:, jj].bitcast(F32), in_=xt_ps[:].rearrange("p g u r -> p g r u")
                 )
             grouped_of[k] = grouped
-            hst_ps = plain_banks.tile([P, 2, 4, P], BF16, tag="plain")
-            for jj in range(2):
-                for w in range(4):
-                    nc.tensor.transpose(hst_ps[:, jj, w, :], side[w][:, 2 * k + jj, :], ident_bf[:])
-            hst = stage.tile([P, 2, 4, P], BF16)
-            nc.scalar.copy(out=hst[:], in_=hst_ps[:])
-            hst_of[k] = hst
 
         def quantise(k):
             codes = work.tile([P, 2, PASSES, P], U32, align_bytes=64)
@@ -245,13 +242,9 @@ def tile_share_lstm_cell_pa_t_kernel(
             return gates_of[k][:, :, D_H * b : D_H * (b + 1)]
 
         def differences(k):
-            diff = work.tile([P, 2, 3, D_H], F32)
-            nc.gpsimd.tensor_tensor(
-                out=diff[:],
-                in0=gates_of[k][:, :, N_CELL:N_ALL].rearrange("p j (b d) -> p j b d", b=3),
-                in1=gate_of(k, 2).unsqueeze(2).to_broadcast([P, 2, 3, D_H]),
-                op=ALU.subtract,
-            )
+            diff = work.tile([P, 3, 2, D_H], F32)
+            for b in range(3):
+                nc.gpsimd.tensor_tensor(out=diff[:, b], in0=gate_of(k, 4 + b), in1=gate_of(k, 2), op=ALU.subtract)
             diff_of[k] = diff
 
         def hidden(k):
@@ -264,15 +257,15 @@ def tile_share_lstm_cell_pa_t_kernel(
                 diff = diff_of[done]
                 tc_m = tc_of[done]
                 s_0 = work.tile([P, 2, D_H], F32)
-                nc.vector.scalar_tensor_tensor(out=s_0[:], in0=diff[:, :, 0, :], scalar=1.0, in1=tc_m[:], op0=ALU.add, op1=ALU.mult)
+                nc.vector.scalar_tensor_tensor(out=s_0[:], in0=diff[:, 0], scalar=1.0, in1=tc_m[:], op0=ALU.add, op1=ALU.mult)
             if k < PAIRS:
                 keep_part = work.tile([P, 2, D_H], F32)
                 nc.vector.tensor_tensor(out=keep_part[:], in0=gate_of(k, 1), in1=side[4][:, 2 * k : 2 * k + 2, :], op=ALU.mult)
             if 0 <= done:
                 rest_1 = work.tile([P, 2, D_H], F32)
-                nc.vector.scalar_tensor_tensor(out=rest_1[:], in0=diff[:, :, 1, :], scalar=2.0, in1=s_0[:], op0=ALU.add, op1=ALU.subtract)
+                nc.vector.scalar_tensor_tensor(out=rest_1[:], in0=diff[:, 1], scalar=2.0, in1=s_0[:], op0=ALU.add, op1=ALU.subtract)
                 rest_2 = work.tile([P, 2, D_H], F32)
-                nc.vector.scalar_tensor_tensor(out=rest_2[:], in0=s_0[:], scalar=-2.0, in1=diff[:, :, 2, :], op0=ALU.mult, op1=ALU.add)
+                nc.vector.scalar_tensor_tensor(out=rest_2[:], in0=s_0[:], scalar=-2.0, in1=diff[:, 2], op0=ALU.mult, op1=ALU.add)
                 s_1 = work.tile([P, 2, D_H], F32)
                 nc.vector.scalar_tensor_tensor(out=s_1[:], in0=rest_1[:], scalar=0.5, in1=tc_m[:], op0=ALU.mult, op1=ALU.mult)
             if k < PAIRS:
@@ -304,7 +297,7 @@ def tile_share_lstm_cell_pa_t_kernel(
                 tc_of[k] = tc_m
 
         for n in range(-3, PAIRS + 1):
-            if 2 <= n + 3 < PAIRS:
+            if 1 <= n + 3 < PAIRS:
                 load(n + 3)
             if 0 <= n < PAIRS:
                 big_product(n)

@@ -244,12 +244,12 @@ def tile_share_lstm_cell_pa_t_kernel(
         def differences(k):
             diff = work.tile([P, 3, 2, D_H], F32)
             for b in range(3):
-                nc.gpsimd.tensor_tensor(out=diff[:, b], in0=gate_of(k, 4 + b), in1=gate_of(k, 2), op=ALU.subtract)
+                nc.vector.tensor_tensor(out=diff[:, b], in0=gate_of(k, 4 + b), in1=gate_of(k, 2), op=ALU.subtract)
             diff_of[k] = diff
 
         def hidden(k):
             h_t = work.tile([P, 2, D_H], F32)
-            nc.gpsimd.tensor_tensor(out=h_t[:], in0=gate_of(k, 2), in1=tc_of[k][:], op=ALU.mult)
+            nc.vector.tensor_tensor(out=h_t[:], in0=gate_of(k, 2), in1=tc_of[k][:], op=ALU.mult)
             nc.sync.dma_start(out=out_rows[0][:, 2 * k : 2 * k + 2, :], in_=h_t[:])
 
         def finish(done, k):

@@ -19,12 +19,15 @@ D_IN = 1024
 D_H = 128
 TILES = BATCH // P
 PAIRS = TILES // 2
+QUAD = 4
+QUADS = TILES // QUAD
+ROWS_Q = QUAD * P
 K_PASS = 512
 PASSES = D_IN // K_PASS
+BLOCKS = 7
 N_CELL = 4 * D_H
 N_SHARE = 3 * D_H
 N_ALL = N_CELL + N_SHARE
-SIDE_CHUNK = 4
 
 FLOPS = 2 * BATCH * (D_IN + D_H) * N_ALL
 
@@ -62,12 +65,11 @@ def tile_share_lstm_cell_pa_t_kernel(
 
     with ExitStack() as ctx:
         keep = ctx.enter_context(tc.tile_pool(name="keep", bufs=1))
-        x_pool = ctx.enter_context(tc.tile_pool(name="x_pool", bufs=4))
-        stage = ctx.enter_context(tc.tile_pool(name="stage", bufs=4))
-        work = ctx.enter_context(tc.tile_pool(name="work", bufs=3))
-        pre_pool = ctx.enter_context(tc.tile_pool(name="pre_pool", bufs=2))
-        mx_banks = ctx.enter_context(tc.psum_pool(name="mx_banks", bufs=4))
-        plain_banks = ctx.enter_context(tc.psum_pool(name="plain_banks", bufs=4))
+        x_pool = ctx.enter_context(tc.tile_pool(name="x_pool", bufs=3))
+        hst_pool = ctx.enter_context(tc.tile_pool(name="hst_pool", bufs=6))
+        two = ctx.enter_context(tc.tile_pool(name="two", bufs=2))
+        rot = ctx.enter_context(tc.psum_pool(name="rot", bufs=4))
+        pre = ctx.enter_context(tc.psum_pool(name="pre", bufs=4))
 
         side = [keep.tile([P, TILES, D_H], BF16, name="side%d" % w) for w in range(5)]
 
@@ -76,28 +78,36 @@ def tile_share_lstm_cell_pa_t_kernel(
         grouped_of = {}
         codes_of = {}
         scales_of = {}
-        lin_of = {}
-        cell_ps_of = {}
-        mx_ps_of = {}
+        pre_t_of = {}
+        pre_ps_of = {}
         gates_of = {}
         diff_of = {}
-        tc_of = {}
+        tail_of = {}
 
-        def load(k):
-            x_sb = x_pool.tile([P, 2, D_IN], BF16)
-            nc.sync.dma_start(out=x_sb[:], in_=x_rows[:, 2 * k : 2 * k + 2, :])
-            x_of[k] = x_sb
-            if (2 * k) % SIDE_CHUNK == 0:
-                rows = slice(2 * k, 2 * k + SIDE_CHUNK)
-                for w in range(5):
-                    nc.sync.dma_start(out=side[w][:, rows, :], in_=side_rows[w][:, rows, :])
+        def load_x(q, first, count):
+            if first == 0:
+                x_sb = x_pool.tile([P, QUAD, D_IN], BF16, name="x_sb")
+                x_of[q] = x_sb
+            nc.sync.dma_start(
+                out=x_of[q][:, first : first + count, :], in_=x_rows[:, QUAD * q + first : QUAD * q + first + count, :]
+            )
 
-        w_small_rows = keep.tile([P, 7, D_H], BF16)
+        def load_side(q, which):
+            rows = slice(QUAD * q, QUAD * (q + 1))
+            for w in which:
+                nc.sync.dma_start(out=side[w][:, rows, :], in_=side_rows[w][:, rows, :])
+
+        warm = keep.tile([P, 2], F32)
+        nc.vector.memset(warm[:], 0.0)
+        nc.scalar.activation(out=warm[:, 1:2], in_=warm[:, 0:1], func=ACT.Sigmoid)
+
+        w_small_rows = keep.tile([P, BLOCKS, D_H], BF16)
         nc.scalar.dma_start(out=w_small_rows[:, 0:4, :], in_=weight_hh.rearrange("(b c) k -> c b k", c=P))
         for b, w_sh in enumerate((weight_sh0, weight_sh1, weight_sh2)):
             nc.scalar.dma_start(out=w_small_rows[:, 4 + b, :], in_=w_sh)
 
-        load(0)
+        load_x(0, 0, 2)
+        load_x(0, 2, 2)
 
         w_words = keep.tile([P, PASSES, 2 * N_ALL], U8, align_bytes=64)
         nc.sync.dma_start(
@@ -113,17 +123,19 @@ def tile_share_lstm_cell_pa_t_kernel(
                 .rearrange("g r n -> r g n")
                 .bitcast(I32),
             )
+        load_side(0, (0, 1, 2, 3))
+        load_x(1, 0, 2)
+        load_x(1, 2, 2)
+        load_side(0, (4,))
+        load_side(1, (0, 1, 2, 3, 4))
+        load_x(2, 0, 4)
 
-        bias_rows = keep.tile([P, N_ALL], BF16)
+        bias_rows = keep.tile([P, D_H], BF16)
         nc.vector.memset(bias_rows[:], 0.0)
-        nc.scalar.dma_start(out=bias_rows[0:1, :], in_=bias_ih.unsqueeze(0))
-        nc.scalar.dma_start(out=bias_rows[1:2, 0:N_CELL], in_=bias_hh.unsqueeze(0))
+        nc.scalar.dma_start(out=bias_rows[0:7, :], in_=bias_ih.rearrange("(b c) -> b c", c=D_H))
+        nc.scalar.dma_start(out=bias_rows[7:11, :], in_=bias_hh.rearrange("(b c) -> b c", c=D_H))
         for b, b_sh in enumerate((bias_sh0, bias_sh1, bias_sh2)):
-            nc.scalar.dma_start(
-                out=bias_rows[1:2, N_CELL + D_H * b : N_CELL + D_H * (b + 1)], in_=b_sh.unsqueeze(0)
-            )
-        ones = keep.tile([P, P], BF16)
-        nc.vector.memset(ones[:], 1.0)
+            nc.scalar.dma_start(out=bias_rows[11 + b : 12 + b, :], in_=b_sh.unsqueeze(0))
 
         ident_f32 = keep.tile([P, P], F32)
         make_identity(nc, ident_f32[:])
@@ -136,185 +148,228 @@ def tile_share_lstm_cell_pa_t_kernel(
         nc.gpsimd.tensor_copy(out=mask_f32[:], in_=mask_bf[:])
 
         w_small = keep.tile([P, N_ALL], BF16)
-        w_small_ps = plain_banks.tile([P, 7, D_H], BF16, tag="plain")
-        for b in range(7):
+        w_small_ps = rot.tile([P, BLOCKS, D_H], BF16, tag="rot")
+        for b in range(BLOCKS):
             nc.tensor.transpose(w_small_ps[:, b, :], w_small_rows[:, b, :], ident_bf[:])
         nc.scalar.copy(out=w_small[:], in_=w_small_ps[:].rearrange("k b c -> k (b c)"))
 
-        bias_cell = keep.tile([P, N_CELL], F32)
+        bias_ps = rot.tile([P, D_H], BF16, tag="rot")
+        nc.tensor.transpose(bias_ps[:], bias_rows[:], ident_bf[:])
+        bias_parts = keep.tile([P, 2 * BLOCKS], F32)
+        nc.vector.tensor_copy(out=bias_parts[:], in_=bias_ps[:, 0 : 2 * BLOCKS])
+        bias_col = keep.tile([P, BLOCKS], F32)
+        nc.vector.tensor_tensor(
+            out=bias_col[:], in0=bias_parts[:, 0:BLOCKS], in1=bias_parts[:, BLOCKS : 2 * BLOCKS], op=ALU.add
+        )
 
-        def spread_bias():
-            bias_cell_ps = plain_banks.tile([P, N_CELL], F32, tag="plain")
-            nc.tensor.matmul(bias_cell_ps[:], lhsT=ones[:], rhs=bias_rows[:, 0:N_CELL], start=True, stop=True)
-            nc.vector.tensor_copy(out=bias_cell[:], in_=bias_cell_ps[:])
-
-        def front(k):
-            hst_ps = plain_banks.tile([P, 2, 4, P], BF16, tag="plain")
+        def turn_side(n, engine):
+            hst_ps = rot.tile([P, 2, 4, P], BF16, tag="rot")
             for jj in range(2):
                 for w in range(4):
-                    nc.tensor.transpose(hst_ps[:, jj, w, :], side[w][:, 2 * k + jj, :], ident_bf[:])
-            hst = stage.tile([P, 2, 4, P], BF16)
-            nc.scalar.copy(out=hst[:], in_=hst_ps[:])
-            hst_of[k] = hst
-            grouped = stage.tile([P, 2, PASSES, P, 4], BF16, align_bytes=64)
-            for jj in range(2):
-                x_words = x_of[k][:, jj, :].bitcast(F32)
-                xt_ps = plain_banks.tile([P, PASSES, 2, P], F32, tag="plain")
-                for g in range(PASSES):
-                    for u in range(2):
-                        nc.tensor.transpose(
-                            xt_ps[:, g, u, :], x_words[:, 256 * g + u : 256 * (g + 1) : 2], ident_f32[:]
-                        )
-                nc.scalar.copy(
-                    out=grouped[:, jj].bitcast(F32), in_=xt_ps[:].rearrange("p g u r -> p g r u")
-                )
-            grouped_of[k] = grouped
+                    nc.tensor.transpose(hst_ps[:, jj, w, :], side[w][:, 2 * n + jj, :], ident_bf[:])
+            hst = hst_pool.tile([P, 2, 4, P], BF16)
+            if engine == "vector":
+                nc.vector.tensor_copy(out=hst[:], in_=hst_ps[:])
+            else:
+                nc.scalar.copy(out=hst[:], in_=hst_ps[:])
+            hst_of[n] = hst
 
-        def quantise(k):
-            codes = work.tile([P, 2, PASSES, P], U32, align_bytes=64)
-            scales = work.tile([P, 2, PASSES, P], U8, align_bytes=64)
-            nc.vector.quantize_mx(
-                out=codes[:].rearrange("p j g r -> p (j g r)").bitcast(FP8X4),
-                scales=scales[:].rearrange("p j g r -> p (j g r)"),
-                in_=grouped_of[k][:].rearrange("p j g r t -> p (j g r t)"),
-            )
-            codes_of[k] = codes
-            scales_of[k] = scales
-
-        def small_products(k):
-            lin = work.tile([P, 2, N_ALL], F32)
-            lin_of[k] = lin
-            hst = hst_of[k]
-            for jj in range(2):
-                cell_ps = plain_banks.tile([P, N_CELL], F32, tag="plain")
-                nc.tensor.matmul(cell_ps[:], lhsT=hst[:, jj, 0, :], rhs=w_small[:, 0:N_CELL], start=True, stop=True)
-                cell_ps_of[(k, jj)] = cell_ps
-                share_ps = plain_banks.tile([P, N_SHARE], F32, tag="plain")
-                for b in range(3):
-                    cols = slice(N_CELL + D_H * b, N_CELL + D_H * (b + 1))
-                    acc = share_ps[:, D_H * b : D_H * (b + 1)]
-                    nc.tensor.matmul(acc, lhsT=ones[:], rhs=bias_rows[:, cols], start=True, stop=False)
-                    nc.tensor.matmul(acc, lhsT=hst[:, jj, 1 + b, :], rhs=w_small[:, cols], start=False, stop=True)
-                nc.scalar.copy(out=lin[:, jj, N_CELL:N_ALL], in_=share_ps[:])
-
-        def cell_bias(k, jj):
-            nc.vector.tensor_tensor(
-                out=lin_of[k][:, jj, 0:N_CELL], in0=cell_ps_of[(k, jj)][:], in1=bias_cell[:], op=ALU.add
-            )
-
-        def mx_group(acc, k, jj, first, width):
+        def turn_x(tile, engine):
+            q, t = divmod(tile, QUAD)
+            if t == 0:
+                grouped = two.tile([P, PASSES, QUAD, P, 4], BF16, align_bytes=64)
+                grouped_of[q] = grouped
+            x_words = x_of[q][:, t, :].bitcast(F32)
+            xt_ps = rot.tile([P, PASSES, 2, P], F32, tag="rot")
             for g in range(PASSES):
-                nc.tensor.matmul_mx(
-                    out=acc,
-                    lhsT=codes_of[k][:, jj, g, :].bitcast(FP8X4),
-                    lhsT_scale=scales_of[k][:, jj, g, :],
-                    rhs=w_words[:, g, 2 * first : 2 * (first + width)].bitcast(FP4X4),
-                    rhs_scale=w_scales[:, g, first : first + width],
-                    start=(g == 0),
-                    stop=(g == PASSES - 1),
+                for u in range(2):
+                    nc.tensor.transpose(xt_ps[:, g, u, :], x_words[:, 256 * g + u : 256 * (g + 1) : 2], ident_f32[:])
+            if engine == "vector":
+                nc.vector.tensor_copy(
+                    out=grouped_of[q][:, :, t].bitcast(F32), in_=xt_ps[:].rearrange("p g u r -> p g r u")
+                )
+            else:
+                nc.scalar.copy(
+                    out=grouped_of[q][:, :, t].bitcast(F32), in_=xt_ps[:].rearrange("p g u r -> p g r u")
                 )
 
-        def big_product(k):
+        def quantise(q):
+            codes = two.tile([P, PASSES, ROWS_Q], U32, align_bytes=64)
+            scales = two.tile([P, PASSES, ROWS_Q], U8, align_bytes=64)
+            for g in range(PASSES):
+                nc.vector.quantize_mx(
+                    out=codes[:, g, :].bitcast(FP8X4),
+                    scales=scales[:, g, :],
+                    in_=grouped_of[q][:, g].rearrange("p t r e -> p (t r e)"),
+                )
+            codes_of[q] = codes
+            scales_of[q] = scales
+
+        def big_product(q, blocks, on_scalar):
+            if blocks[0] == 0:
+                pre_t = two.tile([P, BLOCKS, ROWS_Q], F32)
+                pre_t_of[q] = pre_t
+            for blk in blocks:
+                acc = rot.tile([P, ROWS_Q], F32, tag="rot")
+                for g in range(PASSES):
+                    nc.tensor.matmul_mx(
+                        out=acc[:],
+                        lhsT=w_words[:, g, 2 * D_H * blk : 2 * D_H * (blk + 1)].bitcast(FP4X4),
+                        lhsT_scale=w_scales[:, g, D_H * blk : D_H * (blk + 1)],
+                        rhs=codes_of[q][:, g, :].bitcast(FP8X4),
+                        rhs_scale=scales_of[q][:, g, :],
+                        start=(g == 0),
+                        stop=(g == PASSES - 1),
+                    )
+                if blk in on_scalar:
+                    nc.scalar.activation(
+                        out=pre_t_of[q][:, blk, :], in_=acc[:], func=ACT.Identity, bias=bias_col[:, blk : blk + 1], scale=1.0
+                    )
+                else:
+                    nc.vector.tensor_scalar(
+                        out=pre_t_of[q][:, blk, :], in0=acc[:], scalar1=bias_col[:, blk : blk + 1], scalar2=None, op0=ALU.add
+                    )
+
+        def add_turned(acc, q, t, blk, last):
+            nc.tensor.matmul(
+                acc,
+                lhsT=pre_t_of[q][:, blk, P * t : P * (t + 1)],
+                rhs=ident_f32[:],
+                is_transpose=True,
+                start=False,
+                stop=last,
+            )
+
+        def final(n):
+            q, half = divmod(n, 2)
+            hst = hst_of[n]
+            if half == 0:
+                gates = two.tile([P, QUAD, N_ALL], F32)
+                gates_of[q] = gates
+            gates = gates_of[q]
             for jj in range(2):
-                mx_cell_ps = mx_banks.tile([P, N_CELL], F32, tag="mx")
-                mx_group(mx_cell_ps[:], k, jj, 0, N_CELL)
-                mx_share_ps = mx_banks.tile([P, N_SHARE], F32, tag="mx")
+                t = 2 * half + jj
+                cell_ps = pre.tile([P, N_CELL], F32, tag="pre")
+                nc.tensor.matmul(cell_ps[:], lhsT=hst[:, jj, 0, :], rhs=w_small[:, 0:N_CELL], start=True, stop=False)
+                for blk in range(4):
+                    add_turned(cell_ps[:, D_H * blk : D_H * (blk + 1)], q, t, blk, blk == 3)
+                share_ps = pre.tile([P, N_SHARE], F32, tag="pre")
                 for b in range(3):
-                    mx_group(mx_share_ps[:, D_H * b : D_H * (b + 1)], k, jj, N_CELL + D_H * b, D_H)
-                mx_ps_of[(k, jj)] = (mx_cell_ps, mx_share_ps)
+                    acc = share_ps[:, D_H * b : D_H * (b + 1)]
+                    cols = slice(N_CELL + D_H * b, N_CELL + D_H * (b + 1))
+                    nc.tensor.matmul(acc, lhsT=hst[:, jj, 1 + b, :], rhs=w_small[:, cols], start=True, stop=False)
+                    add_turned(acc, q, t, 4 + b, True)
+                nc.scalar.activation(out=gates[:, t, 0 : 3 * D_H], in_=cell_ps[:, 0 : 3 * D_H], func=ACT.Sigmoid)
+                nc.scalar.activation(out=gates[:, t, 3 * D_H : N_CELL], in_=cell_ps[:, 3 * D_H : N_CELL], func=ACT.Tanh)
+                nc.scalar.activation(out=gates[:, t, N_CELL:N_ALL], in_=share_ps[:], func=ACT.Sigmoid)
 
-        def activate(k):
-            pre = pre_pool.tile([P, 2, N_ALL], F32)
-            gates = work.tile([P, 2, N_ALL], F32)
-            gates_of[k] = gates
-            lin = lin_of[k]
-            for jj in range(2):
-                mx_cell_ps, mx_share_ps = mx_ps_of[(k, jj)]
-                nc.vector.tensor_tensor(out=pre[:, jj, 0:N_CELL], in0=mx_cell_ps[:], in1=lin[:, jj, 0:N_CELL], op=ALU.add)
-                nc.vector.tensor_tensor(
-                    out=pre[:, jj, N_CELL:N_ALL], in0=mx_share_ps[:], in1=lin[:, jj, N_CELL:N_ALL], op=ALU.add
+        def tail_tile(q, name):
+            key = (q, name)
+            if key not in tail_of:
+                tail_of[key] = two.tile([P, QUAD, D_H], F32, name=name)
+            return tail_of[key]
+
+        def differences(q, t0, cnt, engine):
+            gates = gates_of[q]
+            ts = slice(t0, t0 + cnt)
+            if t0 == 0:
+                diff = two.tile([P, QUAD, 3, D_H], F32)
+                diff_of[q] = diff
+            (nc.gpsimd if engine == "gpsimd" else nc.vector).tensor_tensor(
+                out=diff_of[q][:, ts],
+                in0=gates[:, ts, N_CELL:N_ALL].rearrange("p t (b d) -> p t b d", b=3),
+                in1=gates[:, ts, 2 * D_H : 3 * D_H].unsqueeze(2).to_broadcast([P, cnt, 3, D_H]),
+                op=ALU.subtract,
+            )
+
+        def cell_sum(q, t0, cnt):
+            gates = gates_of[q]
+            ts = slice(t0, t0 + cnt)
+            rows = slice(QUAD * q + t0, QUAD * q + t0 + cnt)
+            keep_part = tail_tile(q, "keep_part")
+            in_part = tail_tile(q, "in_part")
+            for t in range(t0, t0 + cnt):
+                m = mask_f32[:, QUAD * q + t : QUAD * q + t + 1]
+                nc.vector.scalar_tensor_tensor(
+                    out=keep_part[:, t, :], in0=gates[:, t, D_H : 2 * D_H], scalar=m, in1=side[4][:, QUAD * q + t, :],
+                    op0=ALU.mult, op1=ALU.mult,
                 )
-                nc.scalar.activation(out=gates[:, jj, 0 : 3 * D_H], in_=pre[:, jj, 0 : 3 * D_H], func=ACT.Sigmoid)
-                nc.scalar.activation(out=gates[:, jj, 3 * D_H : N_CELL], in_=pre[:, jj, 3 * D_H : N_CELL], func=ACT.Tanh)
-                nc.scalar.activation(out=gates[:, jj, N_CELL:N_ALL], in_=pre[:, jj, N_CELL:N_ALL], func=ACT.Sigmoid)
+                nc.vector.scalar_tensor_tensor(
+                    out=in_part[:, t, :], in0=gates[:, t, 0:D_H], scalar=m, in1=gates[:, t, 3 * D_H : N_CELL],
+                    op0=ALU.mult, op1=ALU.mult,
+                )
+            c_t = tail_tile(q, "c_t")
+            nc.vector.tensor_tensor(out=c_t[:, ts], in0=keep_part[:, ts], in1=in_part[:, ts], op=ALU.add)
+            nc.sync.dma_start(out=out_rows[1][:, rows, :], in_=c_t[:, ts])
 
-        def gate_of(k, b):
-            return gates_of[k][:, :, D_H * b : D_H * (b + 1)]
+        def cell_tanh(q, t0, cnt):
+            ts = slice(t0, t0 + cnt)
+            c_t = tail_tile(q, "c_t")
+            tanh_c = tail_tile(q, "tanh_c")
+            nc.scalar.activation(out=tanh_c[:, ts], in_=c_t[:, ts], func=ACT.Tanh)
+            tc_m = tail_tile(q, "tc_m")
+            for t in range(t0, t0 + cnt):
+                m = mask_f32[:, QUAD * q + t : QUAD * q + t + 1]
+                nc.scalar.activation(out=tc_m[:, t, :], in_=tanh_c[:, t, :], func=ACT.Copy, scale=m)
 
-        def differences(k):
-            diff = work.tile([P, 3, 2, D_H], F32)
-            for b in range(3):
-                nc.vector.tensor_tensor(out=diff[:, b], in0=gate_of(k, 4 + b), in1=gate_of(k, 2), op=ALU.subtract)
-            diff_of[k] = diff
+        def outputs(q, t0, cnt):
+            gates = gates_of[q]
+            ts = slice(t0, t0 + cnt)
+            rows = slice(QUAD * q + t0, QUAD * q + t0 + cnt)
+            diff = diff_of[q]
+            tc_m = tail_tile(q, "tc_m")[:, ts]
+            stt = nc.vector.scalar_tensor_tensor
+            s_0 = tail_tile(q, "s_0")[:, ts]
+            stt(out=s_0, in0=diff[:, ts, 0], scalar=1.0, in1=tc_m, op0=ALU.add, op1=ALU.mult)
+            h_t = tail_tile(q, "h_t")[:, ts]
+            nc.vector.tensor_tensor(out=h_t, in0=gates[:, ts, 2 * D_H : 3 * D_H], in1=tc_m, op=ALU.mult)
+            rest_1 = tail_tile(q, "rest_1")[:, ts]
+            stt(out=rest_1, in0=diff[:, ts, 1], scalar=2.0, in1=s_0, op0=ALU.add, op1=ALU.subtract)
+            rest_2 = tail_tile(q, "rest_2")[:, ts]
+            stt(out=rest_2, in0=s_0, scalar=-2.0, in1=diff[:, ts, 2], op0=ALU.mult, op1=ALU.add)
+            s_1 = tail_tile(q, "s_1")[:, ts]
+            stt(out=s_1, in0=rest_1, scalar=0.5, in1=tc_m, op0=ALU.mult, op1=ALU.mult)
+            rest_3 = tail_tile(q, "rest_3")[:, ts]
+            stt(out=rest_3, in0=rest_2, scalar=3.0, in1=s_1, op0=ALU.add, op1=ALU.subtract)
+            s_2 = tail_tile(q, "s_2")[:, ts]
+            stt(out=s_2, in0=rest_3, scalar=1.0 / 3.0, in1=tc_m, op0=ALU.mult, op1=ALU.mult)
+            nc.sync.dma_start(out=out_rows[0][:, rows, :], in_=h_t)
+            nc.sync.dma_start(out=out_rows[2][:, rows, :], in_=s_0)
+            nc.sync.dma_start(out=out_rows[3][:, rows, :], in_=s_1)
+            nc.sync.dma_start(out=out_rows[4][:, rows, :], in_=s_2)
 
-        def hidden(k):
-            h_t = work.tile([P, 2, D_H], F32)
-            nc.vector.tensor_tensor(out=h_t[:], in0=gate_of(k, 2), in1=tc_of[k][:], op=ALU.mult)
-            nc.sync.dma_start(out=out_rows[0][:, 2 * k : 2 * k + 2, :], in_=h_t[:])
-
-        def finish(done, k):
-            if 0 <= done:
-                diff = diff_of[done]
-                tc_m = tc_of[done]
-                s_0 = work.tile([P, 2, D_H], F32)
-                nc.vector.scalar_tensor_tensor(out=s_0[:], in0=diff[:, 0], scalar=1.0, in1=tc_m[:], op0=ALU.add, op1=ALU.mult)
-            if k < PAIRS:
-                keep_part = work.tile([P, 2, D_H], F32)
-                nc.vector.tensor_tensor(out=keep_part[:], in0=gate_of(k, 1), in1=side[4][:, 2 * k : 2 * k + 2, :], op=ALU.mult)
-            if 0 <= done:
-                rest_1 = work.tile([P, 2, D_H], F32)
-                nc.vector.scalar_tensor_tensor(out=rest_1[:], in0=diff[:, 1], scalar=2.0, in1=s_0[:], op0=ALU.add, op1=ALU.subtract)
-                rest_2 = work.tile([P, 2, D_H], F32)
-                nc.vector.scalar_tensor_tensor(out=rest_2[:], in0=s_0[:], scalar=-2.0, in1=diff[:, 2], op0=ALU.mult, op1=ALU.add)
-                s_1 = work.tile([P, 2, D_H], F32)
-                nc.vector.scalar_tensor_tensor(out=s_1[:], in0=rest_1[:], scalar=0.5, in1=tc_m[:], op0=ALU.mult, op1=ALU.mult)
-            if k < PAIRS:
-                in_part = work.tile([P, 2, D_H], F32)
-                nc.vector.tensor_tensor(out=in_part[:], in0=gate_of(k, 0), in1=gate_of(k, 3), op=ALU.mult)
-            if 0 <= done:
-                rest_3 = work.tile([P, 2, D_H], F32)
-                nc.vector.scalar_tensor_tensor(out=rest_3[:], in0=rest_2[:], scalar=3.0, in1=s_1[:], op0=ALU.add, op1=ALU.subtract)
-            if k < PAIRS:
-                c_raw = work.tile([P, 2, D_H], F32)
-                nc.vector.tensor_tensor(out=c_raw[:], in0=in_part[:], in1=keep_part[:], op=ALU.add)
-            if 0 <= done:
-                s_2 = work.tile([P, 2, D_H], F32)
-                nc.vector.scalar_tensor_tensor(out=s_2[:], in0=rest_3[:], scalar=1.0 / 3.0, in1=tc_m[:], op0=ALU.mult, op1=ALU.mult)
-                rows = slice(2 * done, 2 * done + 2)
-                nc.sync.dma_start(out=out_rows[2][:, rows, :], in_=s_0[:])
-                nc.sync.dma_start(out=out_rows[3][:, rows, :], in_=s_1[:])
-                nc.sync.dma_start(out=out_rows[4][:, rows, :], in_=s_2[:])
-            if k < PAIRS:
-                c_t = work.tile([P, 2, D_H], F32)
-                tanh_c = work.tile([P, 2, D_H], F32)
-                tc_m = work.tile([P, 2, D_H], F32)
-                for jj in range(2):
-                    m = mask_f32[:, 2 * k + jj : 2 * k + jj + 1]
-                    nc.scalar.activation(out=tanh_c[:, jj, :], in_=c_raw[:, jj, :], func=ACT.Tanh, scale=m)
-                    nc.scalar.activation(out=tc_m[:, jj, :], in_=tanh_c[:, jj, :], func=ACT.Copy, scale=m)
-                    nc.scalar.activation(out=c_t[:, jj, :], in_=c_raw[:, jj, :], func=ACT.Copy, scale=m)
-                nc.sync.dma_start(out=out_rows[1][:, 2 * k : 2 * k + 2, :], in_=c_t[:])
-                tc_of[k] = tc_m
-
-        for n in range(-3, PAIRS + 1):
-            if 1 <= n + 3 < PAIRS:
-                load(n + 3)
-            if 0 <= n < PAIRS:
-                big_product(n)
-            if 0 <= n + 1 < PAIRS:
-                small_products(n + 1)
-            if 0 <= n < PAIRS:
-                activate(n)
-                differences(n)
-            if n + 1 == 0:
-                spread_bias()
-            if 0 <= n + 1 < PAIRS:
-                cell_bias(n + 1, 0)
-                cell_bias(n + 1, 1)
-                quantise(n + 1)
+        ctx.enter_context(tc.manual_schedule())
+        sums = {}
+        for q in range(QUADS - 2):
+            sums[2 * q + 2] = (q, 0, QUAD)
+        for n in range(PAIRS - 4, PAIRS):
+            sums[n + 1] = (n // 2, 2 * (n % 2), 2)
+        for t in range(4):
+            turn_x(t, "vector" if t % 2 == 0 else "scalar")
+        for n in range(-2, PAIRS + 2):
+            late = n >= PAIRS - 4
+            if n % 2 == 0 and 3 <= (n + 8) // 2 < QUADS:
+                load_x((n + 8) // 2, 0, QUAD)
+            if n % 2 == 0 and 2 <= (n + 6) // 2 < QUADS:
+                load_side((n + 6) // 2, (0, 1, 2, 3, 4))
+            if n in sums:
+                cell_sum(*sums[n])
+            if n % 2 == 0 and 0 <= (n + 2) // 2 < QUADS:
+                quantise((n + 2) // 2)
+            if n - 1 in sums:
+                outputs(*sums[n - 1])
             if 0 <= n + 2 < PAIRS:
-                front(n + 2)
-            if 0 <= n - 1:
-                hidden(n - 1)
-            if 0 <= n:
-                finish(n - 1, n)
+                turn_side(n + 2, "scalar")
+            if 0 <= n < PAIRS:
+                final(n)
+                differences(n // 2, 2 * (n % 2), 2, "gpsimd" if not late else "vector")
+            if n in sums:
+                cell_tanh(*sums[n])
+            if 0 <= n + 2 < PAIRS:
+                if n % 2 == 0:
+                    big_product((n + 2) // 2, (0, 1, 2), (0, 1, 2) if late else ())
+                else:
+                    big_product((n + 2) // 2, (3, 4, 5, 6), (3, 4, 5, 6) if late else (4, 6))
+            if 0 <= n + 4 < PAIRS:
+                turn_x(2 * (n + 4), "scalar")
+                turn_x(2 * (n + 4) + 1, "scalar")

@@ -299,7 +299,8 @@ def tile_share_lstm_cell_pa_t_kernel(
                     op0=ALU.mult, op1=ALU.mult,
                 )
             c_t = tail_tile(q, "c_t")
-            nc.vector.tensor_tensor(out=c_t[:, ts], in0=keep_part[:, ts], in1=in_part[:, ts], op=ALU.add)
+            for hs in (slice(t0, t0 + cnt // 2), slice(t0 + cnt // 2, t0 + cnt)):
+                nc.vector.tensor_tensor(out=c_t[:, hs], in0=keep_part[:, hs], in1=in_part[:, hs], op=ALU.add)
             nc.sync.dma_start(out=out_rows[1][:, rows, :], in_=c_t[:, ts])
 
         def cell_tanh(q, t0, cnt):
@@ -317,26 +318,30 @@ def tile_share_lstm_cell_pa_t_kernel(
             ts = slice(t0, t0 + cnt)
             rows = slice(QUAD * q + t0, QUAD * q + t0 + cnt)
             diff = diff_of[q]
-            tc_m = tail_tile(q, "tc_m")[:, ts]
+            tc_m = tail_tile(q, "tc_m")
             stt = nc.vector.scalar_tensor_tensor
-            s_0 = tail_tile(q, "s_0")[:, ts]
-            stt(out=s_0, in0=diff[:, ts, 0], scalar=1.0, in1=tc_m, op0=ALU.add, op1=ALU.mult)
-            h_t = tail_tile(q, "h_t")[:, ts]
-            nc.vector.tensor_tensor(out=h_t, in0=gates[:, ts, 2 * D_H : 3 * D_H], in1=tc_m, op=ALU.mult)
-            rest_1 = tail_tile(q, "rest_1")[:, ts]
-            stt(out=rest_1, in0=diff[:, ts, 1], scalar=2.0, in1=s_0, op0=ALU.add, op1=ALU.subtract)
-            rest_2 = tail_tile(q, "rest_2")[:, ts]
-            stt(out=rest_2, in0=s_0, scalar=-2.0, in1=diff[:, ts, 2], op0=ALU.mult, op1=ALU.add)
-            s_1 = tail_tile(q, "s_1")[:, ts]
-            stt(out=s_1, in0=rest_1, scalar=0.5, in1=tc_m, op0=ALU.mult, op1=ALU.mult)
-            rest_3 = tail_tile(q, "rest_3")[:, ts]
-            stt(out=rest_3, in0=rest_2, scalar=3.0, in1=s_1, op0=ALU.add, op1=ALU.subtract)
-            s_2 = tail_tile(q, "s_2")[:, ts]
-            stt(out=s_2, in0=rest_3, scalar=1.0 / 3.0, in1=tc_m, op0=ALU.mult, op1=ALU.mult)
-            nc.sync.dma_start(out=out_rows[0][:, rows, :], in_=h_t)
-            nc.sync.dma_start(out=out_rows[2][:, rows, :], in_=s_0)
-            nc.sync.dma_start(out=out_rows[3][:, rows, :], in_=s_1)
-            nc.sync.dma_start(out=out_rows[4][:, rows, :], in_=s_2)
+            s_0 = tail_tile(q, "s_0")
+            h_t = tail_tile(q, "h_t")
+            rest_1 = tail_tile(q, "rest_1")
+            rest_2 = tail_tile(q, "rest_2")
+            s_1 = tail_tile(q, "s_1")
+            rest_3 = tail_tile(q, "rest_3")
+            s_2 = tail_tile(q, "s_2")
+            stt(out=s_0[:, ts], in0=diff[:, ts, 0], scalar=1.0, in1=tc_m[:, ts], op0=ALU.add, op1=ALU.mult)
+            nc.vector.tensor_tensor(out=h_t[:, ts], in0=gates[:, ts, 2 * D_H : 3 * D_H], in1=tc_m[:, ts], op=ALU.mult)
+            stt(out=rest_1[:, ts], in0=diff[:, ts, 1], scalar=2.0, in1=s_0[:, ts], op0=ALU.add, op1=ALU.subtract)
+            stt(out=rest_2[:, ts], in0=s_0[:, ts], scalar=-2.0, in1=diff[:, ts, 2], op0=ALU.mult, op1=ALU.add)
+            halves = (slice(t0, t0 + cnt // 2), slice(t0 + cnt // 2, t0 + cnt))
+            for hs in halves:
+                stt(out=s_1[:, hs], in0=rest_1[:, hs], scalar=0.5, in1=tc_m[:, hs], op0=ALU.mult, op1=ALU.mult)
+            for hs in halves:
+                stt(out=rest_3[:, hs], in0=rest_2[:, hs], scalar=3.0, in1=s_1[:, hs], op0=ALU.add, op1=ALU.subtract)
+            for hs in halves:
+                stt(out=s_2[:, hs], in0=rest_3[:, hs], scalar=1.0 / 3.0, in1=tc_m[:, hs], op0=ALU.mult, op1=ALU.mult)
+            nc.sync.dma_start(out=out_rows[0][:, rows, :], in_=h_t[:, ts])
+            nc.sync.dma_start(out=out_rows[2][:, rows, :], in_=s_0[:, ts])
+            nc.sync.dma_start(out=out_rows[3][:, rows, :], in_=s_1[:, ts])
+            nc.sync.dma_start(out=out_rows[4][:, rows, :], in_=s_2[:, ts])
 
         ctx.enter_context(tc.manual_schedule())
         sums = {}

@@ -240,28 +240,47 @@ def tile_share_lstm_cell_pa_t_kernel(
                 stop=last,
             )
 
-        def final(n):
-            q, half = divmod(n, 2)
+        def turned(acc, q, t, blk, first, last):
+            nc.tensor.matmul(
+                acc, lhsT=pre_t_of[q][:, blk, P * t : P * (t + 1)], rhs=ident_f32[:], is_transpose=True, start=first, stop=last
+            )
+
+        def banks(n, jj):
+            cell_ps = pre.tile([P, N_CELL], F32, tag="pre")
+            share_ps = pre.tile([P, N_SHARE], F32, tag="pre")
+            pre_ps_of[(n, jj)] = (cell_ps, share_ps)
+
+        def products(n, jj, opens):
+            cell_ps, share_ps = pre_ps_of[(n, jj)]
             hst = hst_of[n]
-            if half == 0:
+            nc.tensor.matmul(cell_ps[:], lhsT=hst[:, jj, 0, :], rhs=w_small[:, 0:N_CELL], start=opens, stop=not opens)
+            for b in range(3):
+                cols = slice(N_CELL + D_H * b, N_CELL + D_H * (b + 1))
+                nc.tensor.matmul(
+                    share_ps[:, D_H * b : D_H * (b + 1)], lhsT=hst[:, jj, 1 + b, :], rhs=w_small[:, cols],
+                    start=(opens and b == 0), stop=(not opens and b == 2),
+                )
+
+        def turns(n, jj, opens):
+            q, half = divmod(n, 2)
+            t = 2 * half + jj
+            cell_ps, share_ps = pre_ps_of[(n, jj)]
+            for blk in range(4):
+                turned(cell_ps[:, D_H * blk : D_H * (blk + 1)], q, t, blk, opens and blk == 0, not opens and blk == 3)
+            for b in range(3):
+                turned(share_ps[:, D_H * b : D_H * (b + 1)], q, t, 4 + b, opens and b == 0, not opens and b == 2)
+
+        def gates_out(n, jj):
+            q, half = divmod(n, 2)
+            t = 2 * half + jj
+            if t == 0:
                 gates = two.tile([P, QUAD, N_ALL], F32)
                 gates_of[q] = gates
             gates = gates_of[q]
-            for jj in range(2):
-                t = 2 * half + jj
-                cell_ps = pre.tile([P, N_CELL], F32, tag="pre")
-                nc.tensor.matmul(cell_ps[:], lhsT=hst[:, jj, 0, :], rhs=w_small[:, 0:N_CELL], start=True, stop=False)
-                for blk in range(4):
-                    add_turned(cell_ps[:, D_H * blk : D_H * (blk + 1)], q, t, blk, blk == 3)
-                share_ps = pre.tile([P, N_SHARE], F32, tag="pre")
-                for b in range(3):
-                    acc = share_ps[:, D_H * b : D_H * (b + 1)]
-                    cols = slice(N_CELL + D_H * b, N_CELL + D_H * (b + 1))
-                    nc.tensor.matmul(acc, lhsT=hst[:, jj, 1 + b, :], rhs=w_small[:, cols], start=True, stop=False)
-                    add_turned(acc, q, t, 4 + b, True)
-                nc.scalar.activation(out=gates[:, t, 0 : 3 * D_H], in_=cell_ps[:, 0 : 3 * D_H], func=ACT.Sigmoid)
-                nc.scalar.activation(out=gates[:, t, 3 * D_H : N_CELL], in_=cell_ps[:, 3 * D_H : N_CELL], func=ACT.Tanh)
-                nc.scalar.activation(out=gates[:, t, N_CELL:N_ALL], in_=share_ps[:], func=ACT.Sigmoid)
+            cell_ps, share_ps = pre_ps_of[(n, jj)]
+            nc.scalar.activation(out=gates[:, t, 0 : 3 * D_H], in_=cell_ps[:, 0 : 3 * D_H], func=ACT.Sigmoid)
+            nc.scalar.activation(out=gates[:, t, 3 * D_H : N_CELL], in_=cell_ps[:, 3 * D_H : N_CELL], func=ACT.Tanh)
+            nc.scalar.activation(out=gates[:, t, N_CELL:N_ALL], in_=share_ps[:], func=ACT.Sigmoid)
 
         def tail_tile(q, name):
             key = (q, name)
@@ -351,22 +370,34 @@ def tile_share_lstm_cell_pa_t_kernel(
             sums[n + 1] = (n // 2, 2 * (n % 2), 2)
         for t in range(4):
             turn_x(t, "vector" if t % 2 == 0 else "scalar")
+        turn_side(0, "scalar")
         for n in range(-2, PAIRS + 2):
             late = n >= PAIRS - 4
             if n % 2 == 0 and 3 <= (n + 8) // 2 < QUADS:
                 load_x((n + 8) // 2, 0, QUAD)
             if n % 2 == 0 and 2 <= (n + 6) // 2 < QUADS:
                 load_side((n + 6) // 2, (0, 1, 2, 3, 4))
-            if n in sums:
-                cell_sum(*sums[n])
             if n % 2 == 0 and 0 <= (n + 2) // 2 < QUADS:
                 quantise((n + 2) // 2)
+            if n in sums:
+                cell_sum(*sums[n])
             if n - 1 in sums:
                 outputs(*sums[n - 1])
-            if 0 <= n + 2 < PAIRS:
-                turn_side(n + 2, "scalar")
             if 0 <= n < PAIRS:
-                final(n)
+                banks(n, 0)
+                products(n, 0, True)
+                turns(n, 0, False)
+                gates_out(n, 0)
+            if 0 <= n + 4 < PAIRS:
+                turn_x(2 * (n + 4), "scalar")
+                turn_x(2 * (n + 4) + 1, "scalar")
+            if 0 <= n + 3 < PAIRS:
+                turn_side(n + 3, "scalar")
+            if 0 <= n < PAIRS:
+                banks(n, 1)
+                turns(n, 1, True)
+                products(n, 1, False)
+                gates_out(n, 1)
                 differences(n // 2, 2 * (n % 2), 2, "gpsimd" if not late else "vector")
             if n in sums:
                 cell_tanh(*sums[n])
@@ -375,6 +406,3 @@ def tile_share_lstm_cell_pa_t_kernel(
                     big_product((n + 2) // 2, (0, 1, 2), (0, 1, 2) if late else ())
                 else:
                     big_product((n + 2) // 2, (3, 4, 5, 6), (3, 4, 5, 6) if late else (4, 6))
-            if 0 <= n + 4 < PAIRS:
-                turn_x(2 * (n + 4), "scalar")
-                turn_x(2 * (n + 4) + 1, "scalar")

@@ -97,25 +97,28 @@ def tile_share_lstm_cell_pa_t_kernel(
             for w in which:
                 nc.sync.dma_start(out=side[w][:, rows, :], in_=side_rows[w][:, rows, :])
 
+        ctx.enter_context(tc.manual_schedule())
+
         warm = keep.tile([P, 2], F32)
         nc.vector.memset(warm[:], 0.0)
         nc.scalar.activation(out=warm[:, 1:2], in_=warm[:, 0:1], func=ACT.Sigmoid)
+        bias_rows = keep.tile([P, D_H], BF16)
+        nc.vector.memset(bias_rows[:], 0.0)
+        w_scales = keep.tile([P, PASSES, N_ALL], U8, align_bytes=64)
+        nc.vector.memset(w_scales[:].bitcast(I32), 0)
+        ident_f32 = keep.tile([P, P], F32)
+        make_identity(nc, ident_f32[:])
+        ident_bf = keep.tile([P, P], BF16)
+        make_identity(nc, ident_bf[:])
 
-        w_small_rows = keep.tile([P, BLOCKS, D_H], BF16)
-        nc.scalar.dma_start(out=w_small_rows[:, 0:4, :], in_=weight_hh.rearrange("(b c) k -> c b k", c=P))
-        for b, w_sh in enumerate((weight_sh0, weight_sh1, weight_sh2)):
-            nc.scalar.dma_start(out=w_small_rows[:, 4 + b, :], in_=w_sh)
-
-        load_x(0, 0, 2)
-        load_x(0, 2, 2)
-
+        for t in range(QUAD):
+            load_x(0, t, 1)
+        load_x(1, 0, 2)
         w_words = keep.tile([P, PASSES, 2 * N_ALL], U8, align_bytes=64)
         nc.sync.dma_start(
             out=w_words[:].bitcast(I32),
             in_=weight_ih_words.rearrange("g p b -> p g b").bitcast(I32),
         )
-        w_scales = keep.tile([P, PASSES, N_ALL], U8, align_bytes=64)
-        nc.vector.memset(w_scales[:].bitcast(I32), 0)
         for quadrant in range(4):
             nc.sync.dma_start(
                 out=w_scales[32 * quadrant : 32 * quadrant + 4, :, :].bitcast(I32),
@@ -123,44 +126,42 @@ def tile_share_lstm_cell_pa_t_kernel(
                 .rearrange("g r n -> r g n")
                 .bitcast(I32),
             )
-        load_side(0, (0, 1, 2, 3))
-        load_x(1, 0, 2)
         load_x(1, 2, 2)
-        load_side(0, (4,))
-        load_side(1, (0, 1, 2, 3, 4))
-        load_x(2, 0, 4)
+        w_small_rows = keep.tile([P, BLOCKS, D_H], BF16)
+        nc.sync.dma_start(out=w_small_rows[:, 0:4, :], in_=weight_hh.rearrange("(b c) k -> c b k", c=P))
+        for b, w_sh in enumerate((weight_sh0, weight_sh1, weight_sh2)):
+            nc.sync.dma_start(out=w_small_rows[:, 4 + b, :], in_=w_sh)
 
-        bias_rows = keep.tile([P, D_H], BF16)
-        nc.vector.memset(bias_rows[:], 0.0)
-        nc.scalar.dma_start(out=bias_rows[0:7, :], in_=bias_ih.rearrange("(b c) -> b c", c=D_H))
-        nc.scalar.dma_start(out=bias_rows[7:11, :], in_=bias_hh.rearrange("(b c) -> b c", c=D_H))
+        nc.gpsimd.dma_start(out=bias_rows[0:7, :], in_=bias_ih.rearrange("(b c) -> b c", c=D_H))
+        nc.gpsimd.dma_start(out=bias_rows[7:11, :], in_=bias_hh.rearrange("(b c) -> b c", c=D_H))
         for b, b_sh in enumerate((bias_sh0, bias_sh1, bias_sh2)):
-            nc.scalar.dma_start(out=bias_rows[11 + b : 12 + b, :], in_=b_sh.unsqueeze(0))
-
-        ident_f32 = keep.tile([P, P], F32)
-        make_identity(nc, ident_f32[:])
-        ident_bf = keep.tile([P, P], BF16)
-        make_identity(nc, ident_bf[:])
-
+            nc.gpsimd.dma_start(out=bias_rows[11 + b : 12 + b, :], in_=b_sh.unsqueeze(0))
         mask_bf = keep.tile([P, TILES], BF16)
-        nc.scalar.dma_start(out=mask_bf[:], in_=mask.rearrange("(p j) -> p j", j=TILES))
+        nc.gpsimd.dma_start(out=mask_bf[:], in_=mask.rearrange("(p j) -> p j", j=TILES))
         mask_f32 = keep.tile([P, TILES], F32)
         nc.gpsimd.tensor_copy(out=mask_f32[:], in_=mask_bf[:])
 
-        w_small = keep.tile([P, N_ALL], BF16)
-        w_small_ps = rot.tile([P, BLOCKS, D_H], BF16, tag="rot")
-        for b in range(BLOCKS):
-            nc.tensor.transpose(w_small_ps[:, b, :], w_small_rows[:, b, :], ident_bf[:])
-        nc.scalar.copy(out=w_small[:], in_=w_small_ps[:].rearrange("k b c -> k (b c)"))
+        load_side(0, (0, 1, 2, 3, 4))
+        load_side(1, (0, 1, 2, 3, 4))
+        load_x(2, 0, 4)
 
-        bias_ps = rot.tile([P, D_H], BF16, tag="rot")
-        nc.tensor.transpose(bias_ps[:], bias_rows[:], ident_bf[:])
+        w_small = keep.tile([P, N_ALL], BF16)
         bias_parts = keep.tile([P, 2 * BLOCKS], F32)
-        nc.vector.tensor_copy(out=bias_parts[:], in_=bias_ps[:, 0 : 2 * BLOCKS])
         bias_col = keep.tile([P, BLOCKS], F32)
-        nc.vector.tensor_tensor(
-            out=bias_col[:], in0=bias_parts[:, 0:BLOCKS], in1=bias_parts[:, BLOCKS : 2 * BLOCKS], op=ALU.add
-        )
+
+        def turn_biases():
+            bias_ps = rot.tile([P, D_H], BF16, tag="rot")
+            nc.tensor.transpose(bias_ps[:], bias_rows[:], ident_bf[:])
+            nc.vector.tensor_copy(out=bias_parts[:], in_=bias_ps[:, 0 : 2 * BLOCKS])
+            nc.vector.tensor_tensor(
+                out=bias_col[:], in0=bias_parts[:, 0:BLOCKS], in1=bias_parts[:, BLOCKS : 2 * BLOCKS], op=ALU.add
+            )
+
+        def turn_small_weights():
+            w_small_ps = rot.tile([P, BLOCKS, D_H], BF16, tag="rot")
+            for b in range(BLOCKS):
+                nc.tensor.transpose(w_small_ps[:, b, :], w_small_rows[:, b, :], ident_bf[:])
+            nc.scalar.copy(out=w_small[:], in_=w_small_ps[:].rearrange("k b c -> k (b c)"))
 
         def turn_side(n, engine):
             hst_ps = rot.tile([P, 2, 4, P], BF16, tag="rot")
@@ -193,15 +194,16 @@ def tile_share_lstm_cell_pa_t_kernel(
                     out=grouped_of[q][:, :, t].bitcast(F32), in_=xt_ps[:].rearrange("p g u r -> p g r u")
                 )
 
-        def quantise(q):
+        def quantise(q, parts):
             codes = two.tile([P, PASSES, ROWS_Q], U32, align_bytes=64)
             scales = two.tile([P, PASSES, ROWS_Q], U8, align_bytes=64)
-            for g in range(PASSES):
-                nc.vector.quantize_mx(
-                    out=codes[:, g, :].bitcast(FP8X4),
-                    scales=scales[:, g, :],
-                    in_=grouped_of[q][:, g].rearrange("p t r e -> p (t r e)"),
-                )
+            for t0, t1 in parts:
+                for g in range(PASSES):
+                    nc.vector.quantize_mx(
+                        out=codes[:, g, P * t0 : P * t1].bitcast(FP8X4),
+                        scales=scales[:, g, P * t0 : P * t1],
+                        in_=grouped_of[q][:, g, t0:t1].rearrange("p t r e -> p (t r e)"),
+                    )
             codes_of[q] = codes
             scales_of[q] = scales
 
@@ -362,38 +364,51 @@ def tile_share_lstm_cell_pa_t_kernel(
             nc.sync.dma_start(out=out_rows[3][:, rows, :], in_=s_1[:, ts])
             nc.sync.dma_start(out=out_rows[4][:, rows, :], in_=s_2[:, ts])
 
-        ctx.enter_context(tc.manual_schedule())
         sums = {}
         for q in range(QUADS - 2):
             sums[2 * q + 2] = (q, 0, QUAD)
         for n in range(PAIRS - 4, PAIRS):
             sums[n + 1] = (n // 2, 2 * (n % 2), 2)
-        for t in range(4):
+
+        for t in range(QUAD):
             turn_x(t, "vector" if t % 2 == 0 else "scalar")
+        quantise(0, ((0, 2), (2, 4)))
+        turn_x(4, "scalar")
+        turn_x(5, "scalar")
+        turn_biases()
+        big_product(0, (0, 1, 2), ())
+        load_side(2, (0, 1, 2, 3, 4))
+        load_x(3, 0, QUAD)
+        big_product(0, (3, 4, 5, 6), (4, 6))
+        turn_x(6, "scalar")
+        turn_x(7, "scalar")
+        turn_small_weights()
         turn_side(0, "scalar")
-        for n in range(-2, PAIRS + 2):
+        turn_side(1, "scalar")
+        turn_side(2, "scalar")
+        for n in range(0, PAIRS + 2):
             late = n >= PAIRS - 4
-            if n % 2 == 0 and 3 <= (n + 8) // 2 < QUADS:
+            if n % 2 == 0 and (n + 8) // 2 < QUADS:
                 load_x((n + 8) // 2, 0, QUAD)
-            if n % 2 == 0 and 2 <= (n + 6) // 2 < QUADS:
+            if n % 2 == 0 and (n + 6) // 2 < QUADS:
                 load_side((n + 6) // 2, (0, 1, 2, 3, 4))
-            if n % 2 == 0 and 0 <= (n + 2) // 2 < QUADS:
-                quantise((n + 2) // 2)
+            if n % 2 == 0 and (n + 2) // 2 < QUADS:
+                quantise((n + 2) // 2, ((0, 4),))
             if n in sums:
                 cell_sum(*sums[n])
             if n - 1 in sums:
                 outputs(*sums[n - 1])
-            if 0 <= n < PAIRS:
+            if n < PAIRS:
                 banks(n, 0)
                 products(n, 0, True)
                 turns(n, 0, False)
                 gates_out(n, 0)
-            if 0 <= n + 4 < PAIRS:
+            if n + 4 < PAIRS:
                 turn_x(2 * (n + 4), "scalar")
                 turn_x(2 * (n + 4) + 1, "scalar")
-            if 0 <= n + 3 < PAIRS:
+            if n + 3 < PAIRS:
                 turn_side(n + 3, "scalar")
-            if 0 <= n < PAIRS:
+            if n < PAIRS:
                 banks(n, 1)
                 turns(n, 1, True)
                 products(n, 1, False)
@@ -401,7 +416,7 @@ def tile_share_lstm_cell_pa_t_kernel(
                 differences(n // 2, 2 * (n % 2), 2, "gpsimd" if not late else "vector")
             if n in sums:
                 cell_tanh(*sums[n])
-            if 0 <= n + 2 < PAIRS:
+            if n + 2 < PAIRS:
                 if n % 2 == 0:
                     big_product((n + 2) // 2, (0, 1, 2), (0, 1, 2) if late else ())
                 else:

@@ -113,6 +113,8 @@ def tile_share_lstm_cell_pa_t_kernel(
 
         for t in range(QUAD):
             load_x(0, t, 1)
+        nc.sync.dma_start(out=bias_rows[0:7, :], in_=bias_ih.rearrange("(b c) -> b c", c=D_H))
+        nc.sync.dma_start(out=bias_rows[7:11, :], in_=bias_hh.rearrange("(b c) -> b c", c=D_H))
         load_x(1, 0, 2)
         w_words = keep.tile([P, PASSES, 2 * N_ALL], U8, align_bytes=64)
         nc.sync.dma_start(
@@ -126,22 +128,21 @@ def tile_share_lstm_cell_pa_t_kernel(
                 .rearrange("g r n -> r g n")
                 .bitcast(I32),
             )
+        for b, b_sh in enumerate((bias_sh0, bias_sh1, bias_sh2)):
+            nc.gpsimd.dma_start(out=bias_rows[11 + b : 12 + b, :], in_=b_sh.unsqueeze(0))
         load_x(1, 2, 2)
         w_small_rows = keep.tile([P, BLOCKS, D_H], BF16)
         nc.sync.dma_start(out=w_small_rows[:, 0:4, :], in_=weight_hh.rearrange("(b c) k -> c b k", c=P))
         for b, w_sh in enumerate((weight_sh0, weight_sh1, weight_sh2)):
             nc.sync.dma_start(out=w_small_rows[:, 4 + b, :], in_=w_sh)
-
-        nc.gpsimd.dma_start(out=bias_rows[0:7, :], in_=bias_ih.rearrange("(b c) -> b c", c=D_H))
-        nc.gpsimd.dma_start(out=bias_rows[7:11, :], in_=bias_hh.rearrange("(b c) -> b c", c=D_H))
-        for b, b_sh in enumerate((bias_sh0, bias_sh1, bias_sh2)):
-            nc.gpsimd.dma_start(out=bias_rows[11 + b : 12 + b, :], in_=b_sh.unsqueeze(0))
+        load_side(0, (0, 1, 2, 3))
         mask_bf = keep.tile([P, TILES], BF16)
-        nc.gpsimd.dma_start(out=mask_bf[:], in_=mask.rearrange("(p j) -> p j", j=TILES))
+        nc.sync.dma_start(out=mask_bf[:], in_=mask.rearrange("(p j) -> p j", j=TILES))
         mask_f32 = keep.tile([P, TILES], F32)
         nc.gpsimd.tensor_copy(out=mask_f32[:], in_=mask_bf[:])
-
-        load_side(0, (0, 1, 2, 3, 4))
+        mask_2 = keep.tile([P, TILES], F32)
+        nc.gpsimd.tensor_scalar(out=mask_2[:], in0=mask_bf[:], scalar1=2.0, scalar2=0.0, op0=ALU.mult, op1=ALU.add)
+        load_side(0, (4,))
         load_side(1, (0, 1, 2, 3, 4))
         load_x(2, 0, 4)
 
@@ -156,12 +157,16 @@ def tile_share_lstm_cell_pa_t_kernel(
             nc.vector.tensor_tensor(
                 out=bias_col[:], in0=bias_parts[:, 0:BLOCKS], in1=bias_parts[:, BLOCKS : 2 * BLOCKS], op=ALU.add
             )
+            nc.vector.tensor_scalar(out=bias_col[:, 3:4], in0=bias_col[:, 3:4], scalar1=2.0, scalar2=None, op0=ALU.mult)
 
         def turn_small_weights():
             w_small_ps = rot.tile([P, BLOCKS, D_H], BF16, tag="rot")
             for b in range(BLOCKS):
                 nc.tensor.transpose(w_small_ps[:, b, :], w_small_rows[:, b, :], ident_bf[:])
-            nc.scalar.copy(out=w_small[:], in_=w_small_ps[:].rearrange("k b c -> k (b c)"))
+            w_rows = w_small_ps[:].rearrange("k b c -> k (b c)")
+            nc.scalar.copy(out=w_small[:, 0 : 3 * D_H], in_=w_rows[:, 0 : 3 * D_H])
+            nc.scalar.activation(out=w_small[:, 3 * D_H : N_CELL], in_=w_rows[:, 3 * D_H : N_CELL], func=ACT.Copy, scale=2.0)
+            nc.scalar.copy(out=w_small[:, N_CELL:N_ALL], in_=w_rows[:, N_CELL:N_ALL])
 
         def turn_side(n, engine):
             hst_ps = rot.tile([P, 2, 4, P], BF16, tag="rot")
@@ -223,13 +228,14 @@ def tile_share_lstm_cell_pa_t_kernel(
                         start=(g == 0),
                         stop=(g == PASSES - 1),
                     )
+                gain = 2.0 if blk == 3 else 1.0
                 if blk in on_scalar:
                     nc.scalar.activation(
-                        out=pre_t_of[q][:, blk, :], in_=acc[:], func=ACT.Identity, bias=bias_col[:, blk : blk + 1], scale=1.0
+                        out=pre_t_of[q][:, blk, :], in_=acc[:], func=ACT.Identity, bias=bias_col[:, blk : blk + 1], scale=gain
                     )
                 else:
                     nc.vector.tensor_scalar(
-                        out=pre_t_of[q][:, blk, :], in0=acc[:], scalar1=bias_col[:, blk : blk + 1], scalar2=None, op0=ALU.add
+                        out=pre_t_of[q][:, blk, :], in0=acc[:], scalar1=gain, scalar2=bias_col[:, blk : blk + 1], op0=ALU.mult, op1=ALU.add
                     )
 
         def add_turned(acc, q, t, blk, last):
@@ -280,8 +286,7 @@ def tile_share_lstm_cell_pa_t_kernel(
                 gates_of[q] = gates
             gates = gates_of[q]
             cell_ps, share_ps = pre_ps_of[(n, jj)]
-            nc.scalar.activation(out=gates[:, t, 0 : 3 * D_H], in_=cell_ps[:, 0 : 3 * D_H], func=ACT.Sigmoid)
-            nc.scalar.activation(out=gates[:, t, 3 * D_H : N_CELL], in_=cell_ps[:, 3 * D_H : N_CELL], func=ACT.Tanh)
+            nc.scalar.activation(out=gates[:, t, 0:N_CELL], in_=cell_ps[:], func=ACT.Sigmoid)
             nc.scalar.activation(out=gates[:, t, N_CELL:N_ALL], in_=share_ps[:], func=ACT.Sigmoid)
 
         def tail_tile(q, name):
@@ -309,19 +314,22 @@ def tile_share_lstm_cell_pa_t_kernel(
             rows = slice(QUAD * q + t0, QUAD * q + t0 + cnt)
             keep_part = tail_tile(q, "keep_part")
             in_part = tail_tile(q, "in_part")
+            nc.vector.scalar_tensor_tensor(
+                out=in_part[:, ts], in0=gates[:, ts, 3 * D_H : N_CELL], scalar=-0.5, in1=gates[:, ts, 0:D_H],
+                op0=ALU.add, op1=ALU.mult,
+            )
             for t in range(t0, t0 + cnt):
                 m = mask_f32[:, QUAD * q + t : QUAD * q + t + 1]
                 nc.vector.scalar_tensor_tensor(
                     out=keep_part[:, t, :], in0=gates[:, t, D_H : 2 * D_H], scalar=m, in1=side[4][:, QUAD * q + t, :],
                     op0=ALU.mult, op1=ALU.mult,
                 )
-                nc.vector.scalar_tensor_tensor(
-                    out=in_part[:, t, :], in0=gates[:, t, 0:D_H], scalar=m, in1=gates[:, t, 3 * D_H : N_CELL],
-                    op0=ALU.mult, op1=ALU.mult,
-                )
             c_t = tail_tile(q, "c_t")
-            for hs in (slice(t0, t0 + cnt // 2), slice(t0 + cnt // 2, t0 + cnt)):
-                nc.vector.tensor_tensor(out=c_t[:, hs], in0=keep_part[:, hs], in1=in_part[:, hs], op=ALU.add)
+            for t in range(t0, t0 + cnt):
+                m2 = mask_2[:, QUAD * q + t : QUAD * q + t + 1]
+                nc.vector.scalar_tensor_tensor(
+                    out=c_t[:, t, :], in0=in_part[:, t, :], scalar=m2, in1=keep_part[:, t, :], op0=ALU.mult, op1=ALU.add,
+                )
             nc.sync.dma_start(out=out_rows[1][:, rows, :], in_=c_t[:, ts])
 
         def cell_tanh(q, t0, cnt):

@@ -28,6 +28,8 @@ BLOCKS = 7
 N_CELL = 4 * D_H
 N_SHARE = 3 * D_H
 N_ALL = N_CELL + N_SHARE
+ON_SCALAR = (4, 6)
+ON_SCALAR_LATE = (1, 4, 5, 6)
 
 FLOPS = 2 * BATCH * (D_IN + D_H) * N_ALL
 
@@ -212,41 +214,31 @@ def tile_share_lstm_cell_pa_t_kernel(
             codes_of[q] = codes
             scales_of[q] = scales
 
-        def big_product(q, blocks, on_scalar):
-            if blocks[0] == 0:
+        def big_block(q, blk, on_scalar):
+            if blk == 0:
                 pre_t = two.tile([P, BLOCKS, ROWS_Q], F32)
                 pre_t_of[q] = pre_t
-            for blk in blocks:
-                acc = rot.tile([P, ROWS_Q], F32, tag="rot")
-                for g in range(PASSES):
-                    nc.tensor.matmul_mx(
-                        out=acc[:],
-                        lhsT=w_words[:, g, 2 * D_H * blk : 2 * D_H * (blk + 1)].bitcast(FP4X4),
-                        lhsT_scale=w_scales[:, g, D_H * blk : D_H * (blk + 1)],
-                        rhs=codes_of[q][:, g, :].bitcast(FP8X4),
-                        rhs_scale=scales_of[q][:, g, :],
-                        start=(g == 0),
-                        stop=(g == PASSES - 1),
-                    )
-                gain = 2.0 if blk == 3 else 1.0
-                if blk in on_scalar:
-                    nc.scalar.activation(
-                        out=pre_t_of[q][:, blk, :], in_=acc[:], func=ACT.Identity, bias=bias_col[:, blk : blk + 1], scale=gain
-                    )
-                else:
-                    nc.vector.tensor_scalar(
-                        out=pre_t_of[q][:, blk, :], in0=acc[:], scalar1=gain, scalar2=bias_col[:, blk : blk + 1], op0=ALU.mult, op1=ALU.add
-                    )
-
-        def add_turned(acc, q, t, blk, last):
-            nc.tensor.matmul(
-                acc,
-                lhsT=pre_t_of[q][:, blk, P * t : P * (t + 1)],
-                rhs=ident_f32[:],
-                is_transpose=True,
-                start=False,
-                stop=last,
-            )
+            acc = rot.tile([P, ROWS_Q], F32, tag="rot")
+            for g in range(PASSES):
+                nc.tensor.matmul_mx(
+                    out=acc[:],
+                    lhsT=w_words[:, g, 2 * D_H * blk : 2 * D_H * (blk + 1)].bitcast(FP4X4),
+                    lhsT_scale=w_scales[:, g, D_H * blk : D_H * (blk + 1)],
+                    rhs=codes_of[q][:, g, :].bitcast(FP8X4),
+                    rhs_scale=scales_of[q][:, g, :],
+                    start=(g == 0),
+                    stop=(g == PASSES - 1),
+                )
+            gain = 2.0 if blk == 3 else 1.0
+            bias = bias_col[:, blk : blk + 1]
+            if on_scalar:
+                nc.scalar.activation(
+                    out=pre_t_of[q][:, blk, :], in_=acc[:], func=ACT.Identity, bias=bias, scale=gain
+                )
+            else:
+                nc.vector.tensor_scalar(
+                    out=pre_t_of[q][:, blk, :], in0=acc[:], scalar1=gain, scalar2=bias, op0=ALU.mult, op1=ALU.add
+                )
 
         def turned(acc, q, t, blk, first, last):
             nc.tensor.matmul(
@@ -295,57 +287,79 @@ def tile_share_lstm_cell_pa_t_kernel(
                 tail_of[key] = two.tile([P, QUAD, D_H], F32, name=name)
             return tail_of[key]
 
-        def differences(q, t0, cnt, engine):
+        def tile_to_gates(tile):
+            n, jj = divmod(tile, 2)
+            banks(n, jj)
+            if jj == 0:
+                products(n, jj, True)
+                turns(n, jj, False)
+            else:
+                turns(n, jj, True)
+                products(n, jj, False)
+            gates_out(n, jj)
+
+        def tail_tile(q, name):
+            key = (q, name)
+            if key not in tail_of:
+                tail_of[key] = two.tile([P, QUAD, D_H], F32, name=name)
+            return tail_of[key]
+
+        def place(n):
+            q, half = divmod(n, 2)
+            return q, slice(2 * half, 2 * half + 2)
+
+        def differences(n, engine):
+            q, ts = place(n)
             gates = gates_of[q]
-            ts = slice(t0, t0 + cnt)
-            if t0 == 0:
+            if n % 2 == 0:
                 diff = two.tile([P, QUAD, 3, D_H], F32)
                 diff_of[q] = diff
-            (nc.gpsimd if engine == "gpsimd" else nc.vector).tensor_tensor(
+            engine.tensor_tensor(
                 out=diff_of[q][:, ts],
                 in0=gates[:, ts, N_CELL:N_ALL].rearrange("p t (b d) -> p t b d", b=3),
-                in1=gates[:, ts, 2 * D_H : 3 * D_H].unsqueeze(2).to_broadcast([P, cnt, 3, D_H]),
+                in1=gates[:, ts, 2 * D_H : 3 * D_H].unsqueeze(2).to_broadcast([P, 2, 3, D_H]),
                 op=ALU.subtract,
             )
 
-        def cell_sum(q, t0, cnt):
-            gates = gates_of[q]
-            ts = slice(t0, t0 + cnt)
-            rows = slice(QUAD * q + t0, QUAD * q + t0 + cnt)
-            keep_part = tail_tile(q, "keep_part")
-            in_part = tail_tile(q, "in_part")
-            nc.vector.scalar_tensor_tensor(
-                out=in_part[:, ts], in0=gates[:, ts, 3 * D_H : N_CELL], scalar=-0.5, in1=gates[:, ts, 0:D_H],
-                op0=ALU.add, op1=ALU.mult,
-            )
-            for t in range(t0, t0 + cnt):
-                m = mask_f32[:, QUAD * q + t : QUAD * q + t + 1]
-                nc.vector.scalar_tensor_tensor(
-                    out=keep_part[:, t, :], in0=gates[:, t, D_H : 2 * D_H], scalar=m, in1=side[4][:, QUAD * q + t, :],
-                    op0=ALU.mult, op1=ALU.mult,
-                )
-            c_t = tail_tile(q, "c_t")
-            for t in range(t0, t0 + cnt):
-                m2 = mask_2[:, QUAD * q + t : QUAD * q + t + 1]
-                nc.vector.scalar_tensor_tensor(
-                    out=c_t[:, t, :], in0=in_part[:, t, :], scalar=m2, in1=keep_part[:, t, :], op0=ALU.mult, op1=ALU.add,
-                )
-            nc.sync.dma_start(out=out_rows[1][:, rows, :], in_=c_t[:, ts])
-
-        def cell_tanh(q, t0, cnt):
-            ts = slice(t0, t0 + cnt)
+        def cell_tanh(n):
+            q, ts = place(n)
             c_t = tail_tile(q, "c_t")
             tanh_c = tail_tile(q, "tanh_c")
             nc.scalar.activation(out=tanh_c[:, ts], in_=c_t[:, ts], func=ACT.Tanh)
             tc_m = tail_tile(q, "tc_m")
-            for t in range(t0, t0 + cnt):
+            for t in range(ts.start, ts.stop):
                 m = mask_f32[:, QUAD * q + t : QUAD * q + t + 1]
                 nc.scalar.activation(out=tc_m[:, t, :], in_=tanh_c[:, t, :], func=ACT.Copy, scale=m)
 
-        def outputs(q, t0, cnt):
+        def cell_parts(tile):
+            q, t = divmod(tile, QUAD)
             gates = gates_of[q]
-            ts = slice(t0, t0 + cnt)
-            rows = slice(QUAD * q + t0, QUAD * q + t0 + cnt)
+            nc.vector.scalar_tensor_tensor(
+                out=tail_tile(q, "in_part")[:, t, :], in0=gates[:, t, 3 * D_H : N_CELL], scalar=-0.5,
+                in1=gates[:, t, 0:D_H], op0=ALU.add, op1=ALU.mult,
+            )
+            nc.vector.scalar_tensor_tensor(
+                out=tail_tile(q, "keep_part")[:, t, :], in0=gates[:, t, D_H : 2 * D_H],
+                scalar=mask_f32[:, tile : tile + 1], in1=side[4][:, tile, :], op0=ALU.mult, op1=ALU.mult,
+            )
+
+        def cell_total(tile):
+            q, t = divmod(tile, QUAD)
+            nc.vector.scalar_tensor_tensor(
+                out=tail_tile(q, "c_t")[:, t, :], in0=tail_tile(q, "in_part")[:, t, :],
+                scalar=mask_2[:, tile : tile + 1], in1=tail_tile(q, "keep_part")[:, t, :],
+                op0=ALU.mult, op1=ALU.add,
+            )
+
+        def store_cell(n):
+            q, ts = place(n)
+            rows = slice(2 * n, 2 * n + 2)
+            nc.sync.dma_start(out=out_rows[1][:, rows, :], in_=tail_tile(q, "c_t")[:, ts])
+
+        def output_steps(n):
+            q, ts = place(n)
+            rows = slice(QUAD * q + ts.start, QUAD * q + ts.stop)
+            gates = gates_of[q]
             diff = diff_of[q]
             tc_m = tail_tile(q, "tc_m")
             stt = nc.vector.scalar_tensor_tensor
@@ -356,76 +370,114 @@ def tile_share_lstm_cell_pa_t_kernel(
             s_1 = tail_tile(q, "s_1")
             rest_3 = tail_tile(q, "rest_3")
             s_2 = tail_tile(q, "s_2")
-            stt(out=s_0[:, ts], in0=diff[:, ts, 0], scalar=1.0, in1=tc_m[:, ts], op0=ALU.add, op1=ALU.mult)
-            nc.vector.tensor_tensor(out=h_t[:, ts], in0=gates[:, ts, 2 * D_H : 3 * D_H], in1=tc_m[:, ts], op=ALU.mult)
-            stt(out=rest_1[:, ts], in0=diff[:, ts, 1], scalar=2.0, in1=s_0[:, ts], op0=ALU.add, op1=ALU.subtract)
-            stt(out=rest_2[:, ts], in0=s_0[:, ts], scalar=-2.0, in1=diff[:, ts, 2], op0=ALU.mult, op1=ALU.add)
-            halves = (slice(t0, t0 + cnt // 2), slice(t0 + cnt // 2, t0 + cnt))
-            for hs in halves:
-                stt(out=s_1[:, hs], in0=rest_1[:, hs], scalar=0.5, in1=tc_m[:, hs], op0=ALU.mult, op1=ALU.mult)
-            for hs in halves:
-                stt(out=rest_3[:, hs], in0=rest_2[:, hs], scalar=3.0, in1=s_1[:, hs], op0=ALU.add, op1=ALU.subtract)
-            for hs in halves:
-                stt(out=s_2[:, hs], in0=rest_3[:, hs], scalar=1.0 / 3.0, in1=tc_m[:, hs], op0=ALU.mult, op1=ALU.mult)
-            nc.sync.dma_start(out=out_rows[0][:, rows, :], in_=h_t[:, ts])
-            nc.sync.dma_start(out=out_rows[2][:, rows, :], in_=s_0[:, ts])
-            nc.sync.dma_start(out=out_rows[3][:, rows, :], in_=s_1[:, ts])
-            nc.sync.dma_start(out=out_rows[4][:, rows, :], in_=s_2[:, ts])
 
-        sums = {}
-        for q in range(QUADS - 2):
-            sums[2 * q + 2] = (q, 0, QUAD)
-        for n in range(PAIRS - 4, PAIRS):
-            sums[n + 1] = (n // 2, 2 * (n % 2), 2)
+            def store(which, tile):
+                nc.sync.dma_start(out=out_rows[which][:, rows, :], in_=tile[:, ts])
+
+            def first():
+                stt(out=s_0[:, ts], in0=diff[:, ts, 0], scalar=1.0, in1=tc_m[:, ts], op0=ALU.add, op1=ALU.mult)
+                nc.vector.tensor_tensor(
+                    out=h_t[:, ts], in0=gates[:, ts, 2 * D_H : 3 * D_H], in1=tc_m[:, ts], op=ALU.mult
+                )
+                store(2, s_0)
+                store(0, h_t)
+
+            def rests():
+                stt(out=rest_1[:, ts], in0=diff[:, ts, 1], scalar=2.0, in1=s_0[:, ts], op0=ALU.add, op1=ALU.subtract)
+                stt(out=rest_2[:, ts], in0=s_0[:, ts], scalar=-2.0, in1=diff[:, ts, 2], op0=ALU.mult, op1=ALU.add)
+
+            def second():
+                stt(out=s_1[:, ts], in0=rest_1[:, ts], scalar=0.5, in1=tc_m[:, ts], op0=ALU.mult, op1=ALU.mult)
+                store(3, s_1)
+
+            def last_rest():
+                stt(out=rest_3[:, ts], in0=rest_2[:, ts], scalar=3.0, in1=s_1[:, ts], op0=ALU.add, op1=ALU.subtract)
+
+            def third():
+                stt(out=s_2[:, ts], in0=rest_3[:, ts], scalar=1.0 / 3.0, in1=tc_m[:, ts], op0=ALU.mult, op1=ALU.mult)
+                store(4, s_2)
+
+            return [first, rests, second, last_rest, third]
 
         for t in range(QUAD):
             turn_x(t, "vector" if t % 2 == 0 else "scalar")
-        quantise(0, ((0, 2), (2, 4)))
-        turn_x(4, "scalar")
-        turn_x(5, "scalar")
+        turn_x(QUAD, "scalar")
         turn_biases()
-        big_product(0, (0, 1, 2), ())
+        quantise(0, ((0, 2), (2, 4)))
+        for blk in range(4):
+            big_block(0, blk, blk in ON_SCALAR)
         load_side(2, (0, 1, 2, 3, 4))
-        load_x(3, 0, QUAD)
-        big_product(0, (3, 4, 5, 6), (4, 6))
-        turn_x(6, "scalar")
-        turn_x(7, "scalar")
         turn_small_weights()
         turn_side(0, "scalar")
-        turn_side(1, "scalar")
-        turn_side(2, "scalar")
-        for n in range(0, PAIRS + 2):
-            late = n >= PAIRS - 4
-            if n % 2 == 0 and (n + 8) // 2 < QUADS:
-                load_x((n + 8) // 2, 0, QUAD)
-            if n % 2 == 0 and (n + 6) // 2 < QUADS:
-                load_side((n + 6) // 2, (0, 1, 2, 3, 4))
-            if n % 2 == 0 and (n + 2) // 2 < QUADS:
-                quantise((n + 2) // 2, ((0, 4),))
-            if n in sums:
-                cell_sum(*sums[n])
-            if n - 1 in sums:
-                outputs(*sums[n - 1])
-            if n < PAIRS:
-                banks(n, 0)
-                products(n, 0, True)
-                turns(n, 0, False)
-                gates_out(n, 0)
-            if n + 4 < PAIRS:
-                turn_x(2 * (n + 4), "scalar")
-                turn_x(2 * (n + 4) + 1, "scalar")
-            if n + 3 < PAIRS:
-                turn_side(n + 3, "scalar")
-            if n < PAIRS:
-                banks(n, 1)
-                turns(n, 1, True)
-                products(n, 1, False)
-                gates_out(n, 1)
-                differences(n // 2, 2 * (n % 2), 2, "gpsimd" if not late else "vector")
-            if n in sums:
-                cell_tanh(*sums[n])
-            if n + 2 < PAIRS:
-                if n % 2 == 0:
-                    big_product((n + 2) // 2, (0, 1, 2), (0, 1, 2) if late else ())
-                else:
-                    big_product((n + 2) // 2, (3, 4, 5, 6), (3, 4, 5, 6) if late else (4, 6))
+        for blk in range(4, BLOCKS):
+            big_block(0, blk, blk in ON_SCALAR)
+        late_step = None
+        for q in range(QUADS):
+            last = q == QUADS - 1
+            diff_engine = nc.vector if q >= QUADS - 2 else nc.gpsimd
+            a, b = 2 * q, 2 * q + 1
+            tile = QUAD * q
+            before = output_steps(a - 1) if q > 0 else [None] * 5
+
+            def run(step):
+                if step is not None:
+                    step()
+
+            if q + 3 < QUADS:
+                load_x(q + 3, 0, QUAD)
+                load_side(q + 3, (0, 1, 2, 3, 4))
+            if not last:
+                turn_x(tile + QUAD + 1, "scalar")
+            turn_side(b, "scalar")
+            if not last:
+                turn_x(tile + QUAD + 2, "scalar")
+                turn_x(tile + QUAD + 3, "scalar")
+            if q > 0:
+                cell_tanh(a - 1)
+            run(late_step)
+            run(before[0])
+            run(before[1])
+            tile_to_gates(tile)
+            if not last:
+                quantise(q + 1, ((0, QUAD),))
+            tile_to_gates(tile + 1)
+            cell_parts(tile)
+            run(before[2])
+            cell_parts(tile + 1)
+            run(before[3])
+            if q + 2 < QUADS:
+                turn_x(tile + 2 * QUAD, "scalar")
+            if not last:
+                turn_side(a + 2, "scalar")
+            tile_to_gates(tile + 2)
+            cell_total(tile)
+            cell_total(tile + 1)
+            store_cell(a)
+            run(before[4])
+            differences(a, diff_engine)
+            tile_to_gates(tile + 3)
+            scalar_blocks = ON_SCALAR_LATE if q + 1 == QUADS - 1 else ON_SCALAR
+            if not last:
+                big_block(q + 1, 0, 0 in scalar_blocks)
+            cell_tanh(a)
+            if not last:
+                for blk in range(1, 6):
+                    big_block(q + 1, blk, blk in scalar_blocks)
+            cell_parts(tile + 2)
+            cell_parts(tile + 3)
+            if not last:
+                big_block(q + 1, 6, 6 in scalar_blocks)
+            differences(b, diff_engine)
+            now = output_steps(a)
+            now[0]()
+            now[1]()
+            cell_total(tile + 2)
+            now[2]()
+            cell_total(tile + 3)
+            store_cell(b)
+            now[3]()
+            late_step = now[4]
+        cell_tanh(PAIRS - 1)
+        late_step()
+        for step in output_steps(PAIRS - 1):
+            step()

@@ -106,6 +106,8 @@ def tile_share_lstm_cell_pa_t_kernel(
         nc.scalar.activation(out=warm[:, 1:2], in_=warm[:, 0:1], func=ACT.Sigmoid)
         bias_rows = keep.tile([P, D_H], BF16)
         nc.vector.memset(bias_rows[:], 0.0)
+        share_rows = keep.tile([P, D_H], BF16)
+        nc.vector.memset(share_rows[:], 0.0)
         w_scales = keep.tile([P, PASSES, N_ALL], U8, align_bytes=64)
         nc.vector.memset(w_scales[:].bitcast(I32), 0)
         ident_f32 = keep.tile([P, P], F32)
@@ -131,7 +133,7 @@ def tile_share_lstm_cell_pa_t_kernel(
                 .bitcast(I32),
             )
         for b, b_sh in enumerate((bias_sh0, bias_sh1, bias_sh2)):
-            nc.gpsimd.dma_start(out=bias_rows[11 + b : 12 + b, :], in_=b_sh.unsqueeze(0))
+            nc.gpsimd.dma_start(out=share_rows[b : b + 1, :], in_=b_sh.unsqueeze(0))
         load_x(1, 2, 2)
         w_small_rows = keep.tile([P, BLOCKS, D_H], BF16)
         nc.sync.dma_start(out=w_small_rows[:, 0:4, :], in_=weight_hh.rearrange("(b c) k -> c b k", c=P))
@@ -152,14 +154,17 @@ def tile_share_lstm_cell_pa_t_kernel(
         bias_parts = keep.tile([P, 2 * BLOCKS], F32)
         bias_col = keep.tile([P, BLOCKS], F32)
 
-        def turn_biases():
+        def cell_biases():
             bias_ps = rot.tile([P, D_H], BF16, tag="rot")
             nc.tensor.transpose(bias_ps[:], bias_rows[:], ident_bf[:])
-            nc.vector.tensor_copy(out=bias_parts[:], in_=bias_ps[:, 0 : 2 * BLOCKS])
-            nc.vector.tensor_tensor(
-                out=bias_col[:], in0=bias_parts[:, 0:BLOCKS], in1=bias_parts[:, BLOCKS : 2 * BLOCKS], op=ALU.add
-            )
+            nc.vector.tensor_copy(out=bias_parts[:, 0:11], in_=bias_ps[:, 0:11])
+            nc.vector.tensor_tensor(out=bias_col[:, 0:4], in0=bias_parts[:, 0:4], in1=bias_parts[:, 7:11], op=ALU.add)
             nc.vector.tensor_scalar(out=bias_col[:, 3:4], in0=bias_col[:, 3:4], scalar1=2.0, scalar2=None, op0=ALU.mult)
+
+        def share_biases():
+            bias_ps = rot.tile([P, D_H], BF16, tag="rot")
+            nc.tensor.transpose(bias_ps[:], share_rows[:], ident_bf[:])
+            nc.vector.tensor_tensor(out=bias_col[:, 4:7], in0=bias_parts[:, 4:7], in1=bias_ps[:, 0:3], op=ALU.add)
 
         def turn_small_weights():
             w_small_ps = rot.tile([P, BLOCKS, D_H], BF16, tag="rot")
@@ -401,20 +406,21 @@ def tile_share_lstm_cell_pa_t_kernel(
 
         for t in range(QUAD):
             turn_x(t, "vector" if t % 2 == 0 else "scalar")
-        turn_x(QUAD, "scalar")
-        turn_biases()
+        turn_x(4, "scalar")
+        turn_x(5, "scalar")
         quantise(0, ((0, 2), (2, 4)))
+        cell_biases()
         for blk in range(4):
             big_block(0, blk, blk in ON_SCALAR)
         load_side(2, (0, 1, 2, 3, 4))
         turn_small_weights()
         turn_side(0, "scalar")
+        share_biases()
         for blk in range(4, BLOCKS):
             big_block(0, blk, blk in ON_SCALAR)
         late_step = None
         for q in range(QUADS):
             last = q == QUADS - 1
-            diff_engine = nc.vector if q >= QUADS - 2 else nc.gpsimd
             a, b = 2 * q, 2 * q + 1
             tile = QUAD * q
             before = output_steps(a - 1) if q > 0 else [None] * 5
@@ -427,10 +433,9 @@ def tile_share_lstm_cell_pa_t_kernel(
                 load_x(q + 3, 0, QUAD)
                 load_side(q + 3, (0, 1, 2, 3, 4))
             if not last:
-                turn_x(tile + QUAD + 1, "scalar")
+                turn_x(tile + QUAD + 2, "scalar")
             turn_side(b, "scalar")
             if not last:
-                turn_x(tile + QUAD + 2, "scalar")
                 turn_x(tile + QUAD + 3, "scalar")
             if q > 0:
                 cell_tanh(a - 1)
@@ -446,7 +451,8 @@ def tile_share_lstm_cell_pa_t_kernel(
             cell_parts(tile + 1)
             run(before[3])
             if q + 2 < QUADS:
-                turn_x(tile + 2 * QUAD, "scalar")
+                turn_x(tile + 2 * QUAD + 0, "scalar")
+                turn_x(tile + 2 * QUAD + 1, "scalar")
             if not last:
                 turn_side(a + 2, "scalar")
             tile_to_gates(tile + 2)
@@ -454,7 +460,7 @@ def tile_share_lstm_cell_pa_t_kernel(
             cell_total(tile + 1)
             store_cell(a)
             run(before[4])
-            differences(a, diff_engine)
+            differences(a, nc.vector if a >= 13 else nc.gpsimd)
             tile_to_gates(tile + 3)
             scalar_blocks = ON_SCALAR_LATE if q + 1 == QUADS - 1 else ON_SCALAR
             if not last:
@@ -467,14 +473,22 @@ def tile_share_lstm_cell_pa_t_kernel(
             cell_parts(tile + 3)
             if not last:
                 big_block(q + 1, 6, 6 in scalar_blocks)
-            differences(b, diff_engine)
+            if last:
+                cell_total(tile + 2)
+                cell_total(tile + 3)
+                store_cell(b)
+                differences(b, nc.vector)
+            else:
+                differences(b, nc.vector if b >= 13 else nc.gpsimd)
             now = output_steps(a)
             now[0]()
             now[1]()
-            cell_total(tile + 2)
+            if not last:
+                cell_total(tile + 2)
             now[2]()
-            cell_total(tile + 3)
-            store_cell(b)
+            if not last:
+                cell_total(tile + 3)
+                store_cell(b)
             now[3]()
             late_step = now[4]
         cell_tanh(PAIRS - 1)

@@ -134,7 +134,6 @@ def tile_share_lstm_cell_pa_t_kernel(
             )
         for b, b_sh in enumerate((bias_sh0, bias_sh1, bias_sh2)):
             nc.gpsimd.dma_start(out=share_rows[b : b + 1, :], in_=b_sh.unsqueeze(0))
-        load_x(1, 2, 2)
         w_small_rows = keep.tile([P, BLOCKS, D_H], BF16)
         nc.sync.dma_start(out=w_small_rows[:, 0:4, :], in_=weight_hh.rearrange("(b c) k -> c b k", c=P))
         for b, w_sh in enumerate((weight_sh0, weight_sh1, weight_sh2)):
@@ -146,6 +145,7 @@ def tile_share_lstm_cell_pa_t_kernel(
         nc.gpsimd.tensor_copy(out=mask_f32[:], in_=mask_bf[:])
         mask_2 = keep.tile([P, TILES], F32)
         nc.gpsimd.tensor_scalar(out=mask_2[:], in0=mask_bf[:], scalar1=2.0, scalar2=0.0, op0=ALU.mult, op1=ALU.add)
+        load_x(1, 2, 2)
         load_side(0, (4,))
         load_side(1, (0, 1, 2, 3, 4))
         load_x(2, 0, 4)
@@ -292,11 +292,18 @@ def tile_share_lstm_cell_pa_t_kernel(
                 tail_of[key] = two.tile([P, QUAD, D_H], F32, name=name)
             return tail_of[key]
 
-        def tile_to_gates(tile):
+        def open_tile(tile):
             n, jj = divmod(tile, 2)
             banks(n, jj)
+            products(n, jj, True)
+
+        def tile_to_gates(tile):
+            n, jj = divmod(tile, 2)
+            if tile % QUAD != 0:
+                banks(n, jj)
             if jj == 0:
-                products(n, jj, True)
+                if tile % QUAD != 0:
+                    products(n, jj, True)
                 turns(n, jj, False)
             else:
                 turns(n, jj, True)
@@ -330,7 +337,8 @@ def tile_share_lstm_cell_pa_t_kernel(
             q, ts = place(n)
             c_t = tail_tile(q, "c_t")
             tanh_c = tail_tile(q, "tanh_c")
-            nc.scalar.activation(out=tanh_c[:, ts], in_=c_t[:, ts], func=ACT.Tanh)
+            for t in range(ts.start, ts.stop):
+                nc.scalar.activation(out=tanh_c[:, t, :], in_=c_t[:, t, :], func=ACT.Tanh)
             tc_m = tail_tile(q, "tc_m")
             for t in range(ts.start, ts.stop):
                 m = mask_f32[:, QUAD * q + t : QUAD * q + t + 1]
@@ -432,6 +440,7 @@ def tile_share_lstm_cell_pa_t_kernel(
             if q + 3 < QUADS:
                 load_x(q + 3, 0, QUAD)
                 load_side(q + 3, (0, 1, 2, 3, 4))
+            open_tile(tile)
             if not last:
                 turn_x(tile + QUAD + 2, "scalar")
             turn_side(b, "scalar")
@@ -481,17 +490,17 @@ def tile_share_lstm_cell_pa_t_kernel(
             else:
                 differences(b, nc.vector if b >= 13 else nc.gpsimd)
             now = output_steps(a)
+            if last:
+                cell_tanh(b)
+                then = output_steps(b)
+                for step in (now[0], now[1], now[2], then[0], now[3], then[1], now[4], then[2], then[3], then[4]):
+                    step()
+                continue
             now[0]()
             now[1]()
-            if not last:
-                cell_total(tile + 2)
+            cell_total(tile + 2)
             now[2]()
-            if not last:
-                cell_total(tile + 3)
-                store_cell(b)
+            cell_total(tile + 3)
+            store_cell(b)
             now[3]()
             late_step = now[4]
-        cell_tanh(PAIRS - 1)
-        late_step()
-        for step in output_steps(PAIRS - 1):
-            step()

@@ -29,7 +29,7 @@ N_CELL = 4 * D_H
 N_SHARE = 3 * D_H
 N_ALL = N_CELL + N_SHARE
 ON_SCALAR = (4, 6)
-ON_SCALAR_LATE = (1, 4, 5, 6)
+ON_SCALAR_LATE = (3, 4, 5, 6)
 
 FLOPS = 2 * BATCH * (D_IN + D_H) * N_ALL
 
@@ -68,7 +68,8 @@ def tile_share_lstm_cell_pa_t_kernel(
     with ExitStack() as ctx:
         keep = ctx.enter_context(tc.tile_pool(name="keep", bufs=1))
         x_pool = ctx.enter_context(tc.tile_pool(name="x_pool", bufs=3))
-        hst_pool = ctx.enter_context(tc.tile_pool(name="hst_pool", bufs=6))
+        hst_pool = ctx.enter_context(tc.tile_pool(name="hst_pool", bufs=4))
+        sp_pool = ctx.enter_context(tc.tile_pool(name="sp_pool", bufs=2))
         two = ctx.enter_context(tc.tile_pool(name="two", bufs=2))
         rot = ctx.enter_context(tc.psum_pool(name="rot", bufs=4))
         pre = ctx.enter_context(tc.psum_pool(name="pre", bufs=4))
@@ -76,6 +77,7 @@ def tile_share_lstm_cell_pa_t_kernel(
         side = [keep.tile([P, TILES, D_H], BF16, name="side%d" % w) for w in range(5)]
 
         x_of = {}
+        spread_of = {}
         hst_of = {}
         grouped_of = {}
         codes_of = {}
@@ -187,6 +189,14 @@ def tile_share_lstm_cell_pa_t_kernel(
                 nc.scalar.copy(out=hst[:], in_=hst_ps[:])
             hst_of[n] = hst
 
+        def spread_x(tile):
+            q, t = divmod(tile, QUAD)
+            x_sp = sp_pool.tile([P, PASSES, 2, P], F32, name="x_sp")
+            nc.vector.tensor_copy(
+                out=x_sp[:], in_=x_of[q][:, t, :].bitcast(F32).rearrange("r (g p u) -> r g u p", g=PASSES, u=2)
+            )
+            spread_of[tile] = x_sp
+
         def turn_x(tile, engine):
             q, t = divmod(tile, QUAD)
             if t == 0:
@@ -196,7 +206,11 @@ def tile_share_lstm_cell_pa_t_kernel(
             xt_ps = rot.tile([P, PASSES, 2, P], F32, tag="rot")
             for g in range(PASSES):
                 for u in range(2):
-                    nc.tensor.transpose(xt_ps[:, g, u, :], x_words[:, 256 * g + u : 256 * (g + 1) : 2], ident_f32[:])
+                    if tile in spread_of:
+                        words = spread_of[tile][:, g, u, :]
+                    else:
+                        words = x_words[:, 256 * g + u : 256 * (g + 1) : 2]
+                    nc.tensor.transpose(xt_ps[:, g, u, :], words, ident_f32[:])
             if engine == "vector":
                 nc.vector.tensor_copy(
                     out=grouped_of[q][:, :, t].bitcast(F32), in_=xt_ps[:].rearrange("p g u r -> p g r u")
@@ -333,6 +347,17 @@ def tile_share_lstm_cell_pa_t_kernel(
                 op=ALU.subtract,
             )
 
+        def tanh_of(n):
+            q, ts = place(n)
+            for t in range(ts.start, ts.stop):
+                nc.scalar.activation(out=tail_tile(q, "tanh_c")[:, t, :], in_=tail_tile(q, "c_t")[:, t, :], func=ACT.Tanh)
+
+        def mask_of(n):
+            q, ts = place(n)
+            for t in range(ts.start, ts.stop):
+                m = mask_f32[:, QUAD * q + t : QUAD * q + t + 1]
+                nc.scalar.activation(out=tail_tile(q, "tc_m")[:, t, :], in_=tail_tile(q, "tanh_c")[:, t, :], func=ACT.Copy, scale=m)
+
         def cell_tanh(n):
             q, ts = place(n)
             c_t = tail_tile(q, "c_t")
@@ -424,6 +449,8 @@ def tile_share_lstm_cell_pa_t_kernel(
         turn_small_weights()
         turn_side(0, "scalar")
         share_biases()
+        spread_x(6)
+        spread_x(7)
         for blk in range(4, BLOCKS):
             big_block(0, blk, blk in ON_SCALAR)
         late_step = None
@@ -449,11 +476,11 @@ def tile_share_lstm_cell_pa_t_kernel(
             if q > 0:
                 cell_tanh(a - 1)
             run(late_step)
-            run(before[0])
-            run(before[1])
             tile_to_gates(tile)
             if not last:
                 quantise(q + 1, ((0, QUAD),))
+            run(before[0])
+            run(before[1])
             tile_to_gates(tile + 1)
             cell_parts(tile)
             run(before[2])
@@ -474,10 +501,14 @@ def tile_share_lstm_cell_pa_t_kernel(
             scalar_blocks = ON_SCALAR_LATE if q + 1 == QUADS - 1 else ON_SCALAR
             if not last:
                 big_block(q + 1, 0, 0 in scalar_blocks)
-            cell_tanh(a)
-            if not last:
+            tanh_of(a)
+            if last:
+                mask_of(a)
+            else:
                 for blk in range(1, 6):
                     big_block(q + 1, blk, blk in scalar_blocks)
+                    if blk == 4:
+                        mask_of(a)
             cell_parts(tile + 2)
             cell_parts(tile + 3)
             if not last:
@@ -502,5 +533,9 @@ def tile_share_lstm_cell_pa_t_kernel(
             now[2]()
             cell_total(tile + 3)
             store_cell(b)
+            if q + 3 < QUADS:
+                spread_x(tile + 3 * QUAD)
             now[3]()
+            if False and q + 3 < QUADS:
+                spread_x(tile + 3 * QUAD)
             late_step = now[4]

from contextlib import ExitStack

import concourse.mybir as mybir
from concourse.masks import make_identity

F32 = mybir.dt.float32
BF16 = mybir.dt.bfloat16
I32 = mybir.dt.int32
U32 = mybir.dt.uint32
U8 = mybir.dt.uint8
FP8X4 = mybir.dt.float8_e4m3fn_x4
FP4X4 = mybir.dt.float4_e2m1fn_x4
ALU = mybir.AluOpType
ACT = mybir.ActivationFunctionType

P = 128
BATCH = 4096
D_IN = 1024
D_H = 128
TILES = BATCH // P
PAIRS = TILES // 2
QUAD = 4
QUADS = TILES // QUAD
ROWS_Q = QUAD * P
K_PASS = 512
PASSES = D_IN // K_PASS
BLOCKS = 7
N_CELL = 4 * D_H
N_SHARE = 3 * D_H
N_ALL = N_CELL + N_SHARE
ON_SCALAR = (4, 6)
ON_SCALAR_LATE = (3, 4, 5, 6)

FLOPS = 2 * BATCH * (D_IN + D_H) * N_ALL


def tile_share_lstm_cell_pa_t_kernel(
    tc,
    x,
    h_minors,
    c_minors,
    s0,
    s1,
    s2,
    mask,
    weight_ih_words,
    weight_ih_scales,
    bias_ih,
    weight_hh,
    bias_hh,
    weight_sh0,
    bias_sh0,
    weight_sh1,
    bias_sh1,
    weight_sh2,
    bias_sh2,
    out_0,
    out_1,
    out_2,
    out_3,
    out_4,
):
    nc = tc.nc
    x_rows = x.rearrange("(p j) k -> p j k", j=TILES)
    side_rows = [a.rearrange("(p j) d -> p j d", j=TILES) for a in (h_minors, s0, s1, s2, c_minors)]
    out_rows = [a.rearrange("(p j) d -> p j d", j=TILES) for a in (out_0, out_1, out_2, out_3, out_4)]

    with ExitStack() as ctx:
        keep = ctx.enter_context(tc.tile_pool(name="keep", bufs=1))
        x_pool = ctx.enter_context(tc.tile_pool(name="x_pool", bufs=3))
        hst_pool = ctx.enter_context(tc.tile_pool(name="hst_pool", bufs=4))
        sp_pool = ctx.enter_context(tc.tile_pool(name="sp_pool", bufs=2))
        two = ctx.enter_context(tc.tile_pool(name="two", bufs=2))
        rot = ctx.enter_context(tc.psum_pool(name="rot", bufs=4))
        pre = ctx.enter_context(tc.psum_pool(name="pre", bufs=4))

        side = [keep.tile([P, TILES, D_H], BF16, name="side%d" % w) for w in range(5)]

        x_of = {}
        spread_of = {}
        hst_of = {}
        grouped_of = {}
        codes_of = {}
        scales_of = {}
        pre_t_of = {}
        pre_ps_of = {}
        gates_of = {}
        diff_of = {}
        tail_of = {}

        def load_x(q, first, count):
            if first == 0:
                x_sb = x_pool.tile([P, QUAD, D_IN], BF16, name="x_sb")
                x_of[q] = x_sb
            nc.sync.dma_start(
                out=x_of[q][:, first : first + count, :], in_=x_rows[:, QUAD * q + first : QUAD * q + first + count, :]
            )

        def load_side(q, which):
            rows = slice(QUAD * q, QUAD * (q + 1))
            for w in which:
                nc.sync.dma_start(out=side[w][:, rows, :], in_=side_rows[w][:, rows, :])

        ctx.enter_context(tc.manual_schedule())

        warm = keep.tile([P, 2], F32)
        nc.vector.memset(warm[:], 0.0)
        nc.scalar.activation(out=warm[:, 1:2], in_=warm[:, 0:1], func=ACT.Sigmoid)
        bias_rows = keep.tile([P, D_H], BF16)
        nc.vector.memset(bias_rows[:], 0.0)
        share_rows = keep.tile([P, D_H], BF16)
        nc.vector.memset(share_rows[:], 0.0)
        w_scales = keep.tile([P, PASSES, N_ALL], U8, align_bytes=64)
        nc.vector.memset(w_scales[:].bitcast(I32), 0)
        ident_f32 = keep.tile([P, P], F32)
        make_identity(nc, ident_f32[:])
        ident_bf = keep.tile([P, P], BF16)
        make_identity(nc, ident_bf[:])

        for t in range(QUAD):
            load_x(0, t, 1)
        nc.sync.dma_start(out=bias_rows[0:7, :], in_=bias_ih.rearrange("(b c) -> b c", c=D_H))
        nc.sync.dma_start(out=bias_rows[7:11, :], in_=bias_hh.rearrange("(b c) -> b c", c=D_H))
        load_x(1, 0, 2)
        w_words = keep.tile([P, PASSES, 2 * N_ALL], U8, align_bytes=64)
        nc.sync.dma_start(
            out=w_words[:].bitcast(I32),
            in_=weight_ih_words.rearrange("g p b -> p g b").bitcast(I32),
        )
        for quadrant in range(4):
            nc.sync.dma_start(
                out=w_scales[32 * quadrant : 32 * quadrant + 4, :, :].bitcast(I32),
                in_=weight_ih_scales[:, 4 * quadrant : 4 * quadrant + 4, :]
                .rearrange("g r n -> r g n")
                .bitcast(I32),
            )
        for b, b_sh in enumerate((bias_sh0, bias_sh1, bias_sh2)):
            nc.gpsimd.dma_start(out=share_rows[b : b + 1, :], in_=b_sh.unsqueeze(0))
        w_small_rows = keep.tile([P, BLOCKS, D_H], BF16)
        nc.sync.dma_start(out=w_small_rows[:, 0:4, :], in_=weight_hh.rearrange("(b c) k -> c b k", c=P))
        for b, w_sh in enumerate((weight_sh0, weight_sh1, weight_sh2)):
            nc.sync.dma_start(out=w_small_rows[:, 4 + b, :], in_=w_sh)
        load_side(0, (0, 1, 2, 3))
        mask_bf = keep.tile([P, TILES], BF16)
        nc.sync.dma_start(out=mask_bf[:], in_=mask.rearrange("(p j) -> p j", j=TILES))
        mask_f32 = keep.tile([P, TILES], F32)
        nc.gpsimd.tensor_copy(out=mask_f32[:], in_=mask_bf[:])
        mask_2 = keep.tile([P, TILES], F32)
        nc.gpsimd.tensor_scalar(out=mask_2[:], in0=mask_bf[:], scalar1=2.0, scalar2=0.0, op0=ALU.mult, op1=ALU.add)
        load_x(1, 2, 2)
        load_side(0, (4,))
        load_side(1, (0, 1, 2, 3, 4))
        load_x(2, 0, 4)

        w_small = keep.tile([P, N_ALL], BF16)
        bias_parts = keep.tile([P, 2 * BLOCKS], F32)
        bias_col = keep.tile([P, BLOCKS], F32)

        def cell_biases():
            bias_ps = rot.tile([P, D_H], BF16, tag="rot")
            nc.tensor.transpose(bias_ps[:], bias_rows[:], ident_bf[:])
            nc.vector.tensor_copy(out=bias_parts[:, 0:11], in_=bias_ps[:, 0:11])
            nc.vector.tensor_tensor(out=bias_col[:, 0:4], in0=bias_parts[:, 0:4], in1=bias_parts[:, 7:11], op=ALU.add)
            nc.vector.tensor_scalar(out=bias_col[:, 3:4], in0=bias_col[:, 3:4], scalar1=2.0, scalar2=None, op0=ALU.mult)

        def share_biases():
            bias_ps = rot.tile([P, D_H], BF16, tag="rot")
            nc.tensor.transpose(bias_ps[:], share_rows[:], ident_bf[:])
            nc.vector.tensor_tensor(out=bias_col[:, 4:7], in0=bias_parts[:, 4:7], in1=bias_ps[:, 0:3], op=ALU.add)

        def turn_small_weights():
            w_small_ps = rot.tile([P, BLOCKS, D_H], BF16, tag="rot")
            for b in range(BLOCKS):
                nc.tensor.transpose(w_small_ps[:, b, :], w_small_rows[:, b, :], ident_bf[:])
            w_rows = w_small_ps[:].rearrange("k b c -> k (b c)")
            nc.scalar.copy(out=w_small[:, 0 : 3 * D_H], in_=w_rows[:, 0 : 3 * D_H])
            nc.scalar.activation(out=w_small[:, 3 * D_H : N_CELL], in_=w_rows[:, 3 * D_H : N_CELL], func=ACT.Copy, scale=2.0)
            nc.scalar.copy(out=w_small[:, N_CELL:N_ALL], in_=w_rows[:, N_CELL:N_ALL])

        def turn_side(n, engine):
            hst_ps = rot.tile([P, 2, 4, P], BF16, tag="rot")
            for jj in range(2):
                for w in range(4):
                    nc.tensor.transpose(hst_ps[:, jj, w, :], side[w][:, 2 * n + jj, :], ident_bf[:])
            hst = hst_pool.tile([P, 2, 4, P], BF16)
            if engine == "vector":
                nc.vector.tensor_copy(out=hst[:], in_=hst_ps[:])
            else:
                nc.scalar.copy(out=hst[:], in_=hst_ps[:])
            hst_of[n] = hst

        def spread_x(tile):
            q, t = divmod(tile, QUAD)
            x_sp = sp_pool.tile([P, PASSES, 2, P], F32, name="x_sp")
            nc.vector.tensor_copy(
                out=x_sp[:], in_=x_of[q][:, t, :].bitcast(F32).rearrange("r (g p u) -> r g u p", g=PASSES, u=2)
            )
            spread_of[tile] = x_sp

        def turn_x(tile, engine):
            q, t = divmod(tile, QUAD)
            if t == 0:
                grouped = two.tile([P, PASSES, QUAD, P, 4], BF16, align_bytes=64)
                grouped_of[q] = grouped
            x_words = x_of[q][:, t, :].bitcast(F32)
            xt_ps = rot.tile([P, PASSES, 2, P], F32, tag="rot")
            for g in range(PASSES):
                for u in range(2):
                    if tile in spread_of:
                        words = spread_of[tile][:, g, u, :]
                    else:
                        words = x_words[:, 256 * g + u : 256 * (g + 1) : 2]
                    nc.tensor.transpose(xt_ps[:, g, u, :], words, ident_f32[:])
            if engine == "vector":
                nc.vector.tensor_copy(
                    out=grouped_of[q][:, :, t].bitcast(F32), in_=xt_ps[:].rearrange("p g u r -> p g r u")
                )
            else:
                nc.scalar.copy(
                    out=grouped_of[q][:, :, t].bitcast(F32), in_=xt_ps[:].rearrange("p g u r -> p g r u")
                )

        def quantise(q, parts):
            codes = two.tile([P, PASSES, ROWS_Q], U32, align_bytes=64)
            scales = two.tile([P, PASSES, ROWS_Q], U8, align_bytes=64)
            for t0, t1 in parts:
                for g in range(PASSES):
                    nc.vector.quantize_mx(
                        out=codes[:, g, P * t0 : P * t1].bitcast(FP8X4),
                        scales=scales[:, g, P * t0 : P * t1],
                        in_=grouped_of[q][:, g, t0:t1].rearrange("p t r e -> p (t r e)"),
                    )
            codes_of[q] = codes
            scales_of[q] = scales

        def big_block(q, blk, on_scalar):
            if blk == 0:
                pre_t = two.tile([P, BLOCKS, ROWS_Q], F32)
                pre_t_of[q] = pre_t
            acc = rot.tile([P, ROWS_Q], F32, tag="rot")
            for g in range(PASSES):
                nc.tensor.matmul_mx(
                    out=acc[:],
                    lhsT=w_words[:, g, 2 * D_H * blk : 2 * D_H * (blk + 1)].bitcast(FP4X4),
                    lhsT_scale=w_scales[:, g, D_H * blk : D_H * (blk + 1)],
                    rhs=codes_of[q][:, g, :].bitcast(FP8X4),
                    rhs_scale=scales_of[q][:, g, :],
                    start=(g == 0),
                    stop=(g == PASSES - 1),
                )
            gain = 2.0 if blk == 3 else 1.0
            bias = bias_col[:, blk : blk + 1]
            if on_scalar:
                nc.scalar.activation(
                    out=pre_t_of[q][:, blk, :], in_=acc[:], func=ACT.Identity, bias=bias, scale=gain
                )
            else:
                nc.vector.tensor_scalar(
                    out=pre_t_of[q][:, blk, :], in0=acc[:], scalar1=gain, scalar2=bias, op0=ALU.mult, op1=ALU.add
                )

        def turned(acc, q, t, blk, first, last):
            nc.tensor.matmul(
                acc, lhsT=pre_t_of[q][:, blk, P * t : P * (t + 1)], rhs=ident_f32[:], is_transpose=True, start=first, stop=last
            )

        def banks(n, jj):
            cell_ps = pre.tile([P, N_CELL], F32, tag="pre")
            share_ps = pre.tile([P, N_SHARE], F32, tag="pre")
            pre_ps_of[(n, jj)] = (cell_ps, share_ps)

        def products(n, jj, opens):
            cell_ps, share_ps = pre_ps_of[(n, jj)]
            hst = hst_of[n]
            nc.tensor.matmul(cell_ps[:], lhsT=hst[:, jj, 0, :], rhs=w_small[:, 0:N_CELL], start=opens, stop=not opens)
            for b in range(3):
                cols = slice(N_CELL + D_H * b, N_CELL + D_H * (b + 1))
                nc.tensor.matmul(
                    share_ps[:, D_H * b : D_H * (b + 1)], lhsT=hst[:, jj, 1 + b, :], rhs=w_small[:, cols],
                    start=(opens and b == 0), stop=(not opens and b == 2),
                )

        def turns(n, jj, opens):
            q, half = divmod(n, 2)
            t = 2 * half + jj
            cell_ps, share_ps = pre_ps_of[(n, jj)]
            for blk in range(4):
                turned(cell_ps[:, D_H * blk : D_H * (blk + 1)], q, t, blk, opens and blk == 0, not opens and blk == 3)
            for b in range(3):
                turned(share_ps[:, D_H * b : D_H * (b + 1)], q, t, 4 + b, opens and b == 0, not opens and b == 2)

        def gates_out(n, jj):
            q, half = divmod(n, 2)
            t = 2 * half + jj
            if t == 0:
                gates = two.tile([P, QUAD, N_ALL], F32)
                gates_of[q] = gates
            gates = gates_of[q]
            cell_ps, share_ps = pre_ps_of[(n, jj)]
            nc.scalar.activation(out=gates[:, t, 0:N_CELL], in_=cell_ps[:], func=ACT.Sigmoid)
            nc.scalar.activation(out=gates[:, t, N_CELL:N_ALL], in_=share_ps[:], func=ACT.Sigmoid)

        def tail_tile(q, name):
            key = (q, name)
            if key not in tail_of:
                tail_of[key] = two.tile([P, QUAD, D_H], F32, name=name)
            return tail_of[key]

        def open_tile(tile):
            n, jj = divmod(tile, 2)
            banks(n, jj)
            products(n, jj, True)

        def tile_to_gates(tile):
            n, jj = divmod(tile, 2)
            if tile % QUAD != 0:
                banks(n, jj)
            if jj == 0:
                if tile % QUAD != 0:
                    products(n, jj, True)
                turns(n, jj, False)
            else:
                turns(n, jj, True)
                products(n, jj, False)
            gates_out(n, jj)

        def tail_tile(q, name):
            key = (q, name)
            if key not in tail_of:
                tail_of[key] = two.tile([P, QUAD, D_H], F32, name=name)
            return tail_of[key]

        def place(n):
            q, half = divmod(n, 2)
            return q, slice(2 * half, 2 * half + 2)

        def differences(n, engine):
            q, ts = place(n)
            gates = gates_of[q]
            if n % 2 == 0:
                diff = two.tile([P, QUAD, 3, D_H], F32)
                diff_of[q] = diff
            engine.tensor_tensor(
                out=diff_of[q][:, ts],
                in0=gates[:, ts, N_CELL:N_ALL].rearrange("p t (b d) -> p t b d", b=3),
                in1=gates[:, ts, 2 * D_H : 3 * D_H].unsqueeze(2).to_broadcast([P, 2, 3, D_H]),
                op=ALU.subtract,
            )

        def tanh_of(n):
            q, ts = place(n)
            for t in range(ts.start, ts.stop):
                nc.scalar.activation(out=tail_tile(q, "tanh_c")[:, t, :], in_=tail_tile(q, "c_t")[:, t, :], func=ACT.Tanh)

        def mask_of(n):
            q, ts = place(n)
            for t in range(ts.start, ts.stop):
                m = mask_f32[:, QUAD * q + t : QUAD * q + t + 1]
                nc.scalar.activation(out=tail_tile(q, "tc_m")[:, t, :], in_=tail_tile(q, "tanh_c")[:, t, :], func=ACT.Copy, scale=m)

        def cell_tanh(n):
            q, ts = place(n)
            c_t = tail_tile(q, "c_t")
            tanh_c = tail_tile(q, "tanh_c")
            for t in range(ts.start, ts.stop):
                nc.scalar.activation(out=tanh_c[:, t, :], in_=c_t[:, t, :], func=ACT.Tanh)
            tc_m = tail_tile(q, "tc_m")
            for t in range(ts.start, ts.stop):
                m = mask_f32[:, QUAD * q + t : QUAD * q + t + 1]
                nc.scalar.activation(out=tc_m[:, t, :], in_=tanh_c[:, t, :], func=ACT.Copy, scale=m)

        def cell_parts(tile):
            q, t = divmod(tile, QUAD)
            gates = gates_of[q]
            nc.vector.scalar_tensor_tensor(
                out=tail_tile(q, "in_part")[:, t, :], in0=gates[:, t, 3 * D_H : N_CELL], scalar=-0.5,
                in1=gates[:, t, 0:D_H], op0=ALU.add, op1=ALU.mult,
            )
            nc.vector.scalar_tensor_tensor(
                out=tail_tile(q, "keep_part")[:, t, :], in0=gates[:, t, D_H : 2 * D_H],
                scalar=mask_f32[:, tile : tile + 1], in1=side[4][:, tile, :], op0=ALU.mult, op1=ALU.mult,
            )

        def cell_total(tile):
            q, t = divmod(tile, QUAD)
            nc.vector.scalar_tensor_tensor(
                out=tail_tile(q, "c_t")[:, t, :], in0=tail_tile(q, "in_part")[:, t, :],
                scalar=mask_2[:, tile : tile + 1], in1=tail_tile(q, "keep_part")[:, t, :],
                op0=ALU.mult, op1=ALU.add,
            )

        def store_cell(n):
            q, ts = place(n)
            rows = slice(2 * n, 2 * n + 2)
            nc.sync.dma_start(out=out_rows[1][:, rows, :], in_=tail_tile(q, "c_t")[:, ts])

        def output_steps(n):
            q, ts = place(n)
            rows = slice(QUAD * q + ts.start, QUAD * q + ts.stop)
            gates = gates_of[q]
            diff = diff_of[q]
            tc_m = tail_tile(q, "tc_m")
            stt = nc.vector.scalar_tensor_tensor
            s_0 = tail_tile(q, "s_0")
            h_t = tail_tile(q, "h_t")
            rest_1 = tail_tile(q, "rest_1")
            rest_2 = tail_tile(q, "rest_2")
            s_1 = tail_tile(q, "s_1")
            rest_3 = tail_tile(q, "rest_3")
            s_2 = tail_tile(q, "s_2")

            def store(which, tile):
                nc.sync.dma_start(out=out_rows[which][:, rows, :], in_=tile[:, ts])

            def first():
                stt(out=s_0[:, ts], in0=diff[:, ts, 0], scalar=1.0, in1=tc_m[:, ts], op0=ALU.add, op1=ALU.mult)
                nc.vector.tensor_tensor(
                    out=h_t[:, ts], in0=gates[:, ts, 2 * D_H : 3 * D_H], in1=tc_m[:, ts], op=ALU.mult
                )
                store(2, s_0)
                store(0, h_t)

            def rests():
                stt(out=rest_1[:, ts], in0=diff[:, ts, 1], scalar=2.0, in1=s_0[:, ts], op0=ALU.add, op1=ALU.subtract)
                stt(out=rest_2[:, ts], in0=s_0[:, ts], scalar=-2.0, in1=diff[:, ts, 2], op0=ALU.mult, op1=ALU.add)

            def second():
                stt(out=s_1[:, ts], in0=rest_1[:, ts], scalar=0.5, in1=tc_m[:, ts], op0=ALU.mult, op1=ALU.mult)
                store(3, s_1)

            def last_rest():
                stt(out=rest_3[:, ts], in0=rest_2[:, ts], scalar=3.0, in1=s_1[:, ts], op0=ALU.add, op1=ALU.subtract)

            def third():
                stt(out=s_2[:, ts], in0=rest_3[:, ts], scalar=1.0 / 3.0, in1=tc_m[:, ts], op0=ALU.mult, op1=ALU.mult)
                store(4, s_2)

            return [first, rests, second, last_rest, third]

        for t in range(QUAD):
            turn_x(t, "vector" if t % 2 == 0 else "scalar")
        turn_x(4, "scalar")
        turn_x(5, "scalar")
        quantise(0, ((0, 2), (2, 4)))
        cell_biases()
        for blk in range(4):
            big_block(0, blk, blk in ON_SCALAR)
        load_side(2, (0, 1, 2, 3, 4))
        turn_small_weights()
        turn_side(0, "scalar")
        share_biases()
        spread_x(6)
        spread_x(7)
        for blk in range(4, BLOCKS):
            big_block(0, blk, blk in ON_SCALAR)
        late_step = None
        for q in range(QUADS):
            last = q == QUADS - 1
            a, b = 2 * q, 2 * q + 1
            tile = QUAD * q
            before = output_steps(a - 1) if q > 0 else [None] * 5

            def run(step):
                if step is not None:
                    step()

            if q + 3 < QUADS:
                load_x(q + 3, 0, QUAD)
                load_side(q + 3, (0, 1, 2, 3, 4))
            open_tile(tile)
            if not last:
                turn_x(tile + QUAD + 2, "scalar")
            turn_side(b, "scalar")
            if not last:
                turn_x(tile + QUAD + 3, "scalar")
            if q > 0:
                cell_tanh(a - 1)
            run(late_step)
            tile_to_gates(tile)
            if not last:
                quantise(q + 1, ((0, QUAD),))
            run(before[0])
            run(before[1])
            tile_to_gates(tile + 1)
            cell_parts(tile)
            run(before[2])
            cell_parts(tile + 1)
            run(before[3])
            if q + 2 < QUADS:
                turn_x(tile + 2 * QUAD + 0, "scalar")
                turn_x(tile + 2 * QUAD + 1, "scalar")
            if not last:
                turn_side(a + 2, "scalar")
            tile_to_gates(tile + 2)
            cell_total(tile)
            cell_total(tile + 1)
            store_cell(a)
            run(before[4])
            differences(a, nc.vector if a >= 13 else nc.gpsimd)
            tile_to_gates(tile + 3)
            scalar_blocks = ON_SCALAR_LATE if q + 1 == QUADS - 1 else ON_SCALAR
            if not last:
                big_block(q + 1, 0, 0 in scalar_blocks)
            tanh_of(a)
            if last:
                mask_of(a)
            else:
                for blk in range(1, 6):
                    big_block(q + 1, blk, blk in scalar_blocks)
                    if blk == 4:
                        mask_of(a)
            cell_parts(tile + 2)
            cell_parts(tile + 3)
            if not last:
                big_block(q + 1, 6, 6 in scalar_blocks)
            if last:
                cell_total(tile + 2)
                cell_total(tile + 3)
                store_cell(b)
                differences(b, nc.vector)
            else:
                differences(b, nc.vector if b >= 13 else nc.gpsimd)
            now = output_steps(a)
            if last:
                cell_tanh(b)
                then = output_steps(b)
                for step in (now[0], now[1], now[2], then[0], now[3], then[1], now[4], then[2], then[3], then[4]):
                    step()
                continue
            now[0]()
            now[1]()
            cell_total(tile + 2)
            now[2]()
            cell_total(tile + 3)
            store_cell(b)
            if q + 3 < QUADS:
                spread_x(tile + 3 * QUAD)
            now[3]()
            if False and q + 3 < QUADS:
                spread_x(tile + 3 * QUAD)
            late_step = now[4]
